import numpy as np
import ml_dtypes


def mxq(x, axis, fmt="e4m3"):
    dtype, down = {"e4m3": (ml_dtypes.float8_e4m3fn, 7), "e5m2": (ml_dtypes.float8_e5m2, 14)}[fmt]
    v = np.moveaxis(np.asarray(x, np.float32).astype(ml_dtypes.bfloat16).astype(np.float64), axis, -1)
    blocks = v.reshape(v.shape[:-1] + (-1, 32))
    amax = np.abs(blocks).max(-1, keepdims=True)
    byte = np.maximum(np.where(amax > 0, np.frexp(amax)[1] - 1 + 127, 0) - down, 1)
    scale = np.exp2(byte - 127.0)
    codes = (blocks / scale).astype(np.float32).astype(dtype).astype(np.float64)
    return np.moveaxis((codes * scale).reshape(v.shape), -1, axis)


WIDE = False


def mx_kscale(k):
    if not WIDE:
        return np.ones(k)
    levels = np.array([10, -10, 5, -5, 0])
    a = np.random.permutation(np.resize(levels, k // 512 * 4)).reshape(k // 512, 4)
    idx = np.arange(k)
    return np.exp2(a[idx // 512, idx % 128 // 32])


BF16 = ml_dtypes.bfloat16


def bf(x):
    return np.asarray(x, np.float32).astype(BF16)


def f64(x):
    return np.asarray(x).astype(np.float64)


B, V, D, P, Q, R, O = 64, 16, 512, 512, 512, 512, 512
NEG_SLOPE = 0.2


def lrelu(v):
    return np.where(v >= 0, v, NEG_SLOPE * v)


def setup_inputs():
    s, u = mx_kscale(Q), mx_kscale(D + R)
    g = np.random.standard_normal((B, V, V, Q)) * 0.8
    return {"h2": bf(lrelu(g) * s),
            "F": bf(np.random.standard_normal((B, V, D)) * u[:D]),
            "W3": bf(np.random.standard_normal((Q, R)) * 1.5 / np.sqrt(Q) / s[:, None] * u[D:]),
            "b3": bf(np.random.standard_normal(R) * 0.3 * u[D:]),
            "Wf": bf(np.random.standard_normal((D + R, O)) / np.sqrt(D + R) / u[:, None]),
            "b_f": bf(np.random.standard_normal(O) * 0.3)}


def reference(h2, F, W3, b3, Wf, b_f):
    h3 = lrelu((mxq(f64(h2), 3, "e4m3") @ mxq(f64(W3), 0, "e4m3")) + f64(b3))
    Msum = h3.sum(axis=-2)
    X = np.concatenate([f64(F), Msum], axis=-1).reshape(-1, D + R)
    return (mxq(X, 1, "e4m3") @ mxq(f64(Wf), 0, "e4m3")) + f64(b_f)

@@ -1,0 +1,326 @@
+from contextlib import ExitStack
+
+import concourse.mybir as mybir
+from concourse.masks import make_identity
+
+F32 = mybir.dt.float32
+BF16 = mybir.dt.bfloat16
+U32 = mybir.dt.uint32
+U8 = mybir.dt.uint8
+FP8X4 = mybir.dt.float8_e4m3fn_x4
+ALU = mybir.AluOpType
+
+P = 128
+PACK = 4
+K_PASS = P * PACK
+WORDS = K_PASS // 2
+
+VIEWS = 1024
+NEIGH = 16
+Q = 512
+R = 512
+O = 512
+NEG_SLOPE = 0.2
+
+VIEW_TILES = 2
+CHUNK_VIEWS = VIEW_TILES * P
+N_CHUNKS = VIEWS // CHUNK_VIEWS
+UNIT_J = 4
+UNITS_PER_CHUNK = NEIGH // UNIT_J
+N_UNITS = N_CHUNKS * UNITS_PER_CHUNK
+ROW_TILES = VIEW_TILES * UNIT_J
+UNIT_COLS = ROW_TILES * P
+R_BLOCKS = R // P
+BANK = 512
+LOADS_AHEAD = 4
+
+RELU_WEIGHT = 1.0 - NEG_SLOPE
+LINEAR_OVER_RELU = NEG_SLOPE / RELU_WEIGHT
+SEEDS = NEIGH + NEIGH * LINEAR_OVER_RELU
+HALVES = BANK // CHUNK_VIEWS
+
+FLOPS = 2 * VIEWS * NEIGH * Q * R + 2 * VIEWS * (Q + R) * O
+
+
+def tile_nonlocalmp_pb_kernel(tc, h2, feats, W3, b3, Wf, b_f, out):
+    nc = tc.nc
+    h2_rows = h2.rearrange("b i j k -> (b i) j k")
+    feat_rows = feats.rearrange("b i k -> (b i) k")
+
+    with ExitStack() as ctx:
+        consts = ctx.enter_context(tc.tile_pool(name="consts", bufs=1))
+        raw_pool = ctx.enter_context(tc.tile_pool(name="raw", bufs=LOADS_AHEAD + 1))
+        grouped_pool = ctx.enter_context(tc.tile_pool(name="grouped", bufs=3))
+        codes_pool = ctx.enter_context(tc.tile_pool(name="codes", bufs=2))
+        chunk_pool = ctx.enter_context(tc.tile_pool(name="chunk", bufs=2))
+        store_pool = ctx.enter_context(tc.tile_pool(name="store", bufs=3))
+        psum_t = ctx.enter_context(tc.psum_pool(name="psum_t", bufs=3))
+        psum_main = ctx.enter_context(tc.psum_pool(name="psum_main", bufs=3))
+        psum_lin = ctx.enter_context(tc.psum_pool(name="psum_lin", bufs=1))
+        ctx.enter_context(tc.manual_schedule())
+
+        def load_unit(u):
+            c, g = divmod(u, UNITS_PER_CHUNK)
+            raw = raw_pool.tile([P, ROW_TILES * Q], BF16, name="raw")
+            rows = h2_rows[c * CHUNK_VIEWS : (c + 1) * CHUNK_VIEWS, g * UNIT_J : (g + 1) * UNIT_J, :]
+            nc.sync.dma_start(
+                out=raw[:].rearrange("p (t x) -> p t x", t=VIEW_TILES),
+                in_=rows.rearrange("(t p) j k -> p t (j k)", p=P),
+            )
+            return raw
+
+        def spread_k(raw, word_offsets):
+            raw_words = raw[:].bitcast(F32)
+            grouped = grouped_pool.tile([P, UNIT_COLS * PACK], BF16, align_bytes=64, name="grouped")
+            grouped_words = grouped[:].bitcast(F32).rearrange("p (c u) -> p c u", u=2)
+            for pair in range(ROW_TILES // 2):
+                bank = psum_t.tile([P, 2, 2, P], F32, tag="t", name="bank")
+                for s in range(2):
+                    for u in range(2):
+                        first = word_offsets[2 * pair + s] + u * P
+                        nc.tensor.transpose(bank[:, s, u, :], raw_words[:, first : first + P], ident[:])
+                nc.scalar.copy(
+                    out=grouped_words[:, 2 * pair * P : 2 * (pair + 1) * P, :].rearrange(
+                        "p (s r) u -> p s r u", s=2
+                    ),
+                    in_=bank[:].rearrange("p s u r -> p s r u"),
+                )
+            return grouped
+
+        def quantise(grouped_flat, codes_flat, scales_flat):
+            nc.vector.quantize_mx(out=codes_flat.bitcast(FP8X4), scales=scales_flat, in_=grouped_flat)
+
+        def quantise_unit(grouped):
+            codes = codes_pool.tile([P, UNIT_COLS], U32, align_bytes=64, name="codes")
+            scales = codes_pool.tile([P, UNIT_COLS], U8, align_bytes=64, name="scales")
+            quantise(grouped[:], codes[:], scales[:])
+            return codes, scales
+
+        unit_offsets = [(t * UNIT_J + jj) * WORDS for jj in range(UNIT_J) for t in range(VIEW_TILES)]
+
+        ident = consts.tile([P, P], F32, name="ident")
+        make_identity(nc, ident[:])
+        b3_rows = consts.tile([P, P], BF16, name="b3_rows")
+        nc.vector.memset(b3_rows[:], 0.0)
+
+        raws = {0: load_unit(0)}
+        w3_raw = consts.tile([P, PACK, R], BF16, name="w3_raw")
+        nc.sync.dma_start(
+            out=w3_raw[:].rearrange("p (u e) r -> p u (e r)", e=2),
+            in_=W3.rearrange("(u q e) r -> q u (e r)", u=2, e=2),
+        )
+        nc.sync.dma_start(out=b3_rows[0:R_BLOCKS, :], in_=b3.rearrange("(m p) -> m p", p=P))
+        raws[1] = load_unit(1)
+        raws[2] = load_unit(2)
+        feat_raw = consts.tile([P, (VIEWS // P) * Q], BF16, name="feat_raw")
+        nc.sync.dma_start(
+            out=feat_raw[:].rearrange("p (t k) -> p t k", k=Q),
+            in_=feat_rows.rearrange("(t p) k -> p t k", p=P),
+        )
+        wf_raw = consts.tile([P, 2, PACK, O], BF16, name="wf_raw")
+        nc.sync.dma_start(
+            out=wf_raw[:, 0, :, :].rearrange("p (u e) o -> p u (e o)", e=2),
+            in_=Wf[0:K_PASS, :].rearrange("(u q e) o -> q u (e o)", u=2, e=2),
+        )
+        nc.sync.dma_start(
+            out=wf_raw[:, 1, :, :],
+            in_=Wf[K_PASS : 2 * K_PASS, :].rearrange("(t p) o -> p t o", p=P),
+        )
+        bf_all = consts.tile([P, O], BF16, name="bf_all")
+        nc.sync.dma_start(out=bf_all[:], in_=b_f.partition_broadcast(P))
+        raws[3] = load_unit(3)
+
+        grouped_next = spread_k(raws[0], unit_offsets)
+
+        w3_grouped = consts.tile([P, R, PACK], BF16, align_bytes=64, name="w3_grouped")
+        w3_codes = consts.tile([P, R], U32, align_bytes=64, name="w3_codes")
+        w3_scales = consts.tile([P, R], U8, align_bytes=64, name="w3_scales")
+        nc.vector.tensor_copy(out=w3_grouped[:], in_=w3_raw[:].rearrange("p t r -> p r t"))
+        quantise(w3_grouped[:].rearrange("p r t -> p (r t)"), w3_codes[:], w3_scales[:])
+
+        b3_f32 = consts.tile([P, P], F32, name="b3_f32")
+        nc.vector.tensor_copy(out=b3_f32[:], in_=b3_rows[:])
+        b3_bank = psum_t.tile([P, P], F32, tag="t", name="b3_bank")
+        nc.tensor.transpose(b3_bank[:], b3_f32[:], ident[:])
+
+        codes_now, scales_now = quantise_unit(grouped_next)
+
+        neg_b3 = consts.tile([P, R_BLOCKS], F32, name="neg_b3")
+        seed_b3 = consts.tile([P, R_BLOCKS], F32, name="seed_b3")
+        nc.vector.tensor_scalar_mul(out=neg_b3[:], in0=b3_bank[:, 0:R_BLOCKS], scalar1=-1.0)
+        nc.vector.tensor_scalar_mul(out=seed_b3[:], in0=b3_bank[:, 0:R_BLOCKS], scalar1=SEEDS / HALVES)
+
+        feat_codes = consts.tile([P, VIEWS], U32, align_bytes=64, name="feat_codes")
+        feat_scales = consts.tile([P, VIEWS], U8, align_bytes=64, name="feat_scales")
+        wf_grouped = consts.tile([P, 2, O, PACK], BF16, align_bytes=64, name="wf_grouped")
+        wf_codes = consts.tile([P, 2, O], U32, align_bytes=64, name="wf_codes")
+        wf_scales = consts.tile([P, 2, O], U8, align_bytes=64, name="wf_scales")
+
+        relu_sums = {}
+        lin_banks = {}
+        lin_rows = {}
+        folded = {}
+        lin_cols = {}
+        x_grouped = {}
+
+        def message_banks(u, first, last):
+            c, g = divmod(u, UNITS_PER_CHUNK)
+            for i in range(first, last):
+                jp, m = divmod(i, R_BLOCKS)
+                block = slice(m * P, (m + 1) * P)
+                cols = slice(jp * BANK, (jp + 1) * BANK)
+                main = psum_main.tile([P, BANK], F32, name="main")
+                nc.tensor.matmul_mx(
+                    out=main[:],
+                    lhsT=w3_codes[:, block].bitcast(FP8X4),
+                    lhsT_scale=w3_scales[:, block],
+                    rhs=codes_now[:, cols].bitcast(FP8X4),
+                    rhs_scale=scales_now[:, cols],
+                    start=True,
+                    stop=True,
+                )
+                acc = relu_sums[c][:, m, :]
+                if g == 0 and jp == 0:
+                    nc.vector.tensor_scalar(
+                        out=acc,
+                        in0=main[:],
+                        scalar1=neg_b3[:, m : m + 1],
+                        scalar2=seed_b3[:, m : m + 1],
+                        op0=ALU.max,
+                        op1=ALU.add,
+                    )
+                else:
+                    nc.vector.scalar_tensor_tensor(
+                        out=acc,
+                        in0=main[:],
+                        scalar=neg_b3[:, m : m + 1],
+                        in1=acc,
+                        op0=ALU.max,
+                        op1=ALU.add,
+                    )
+                jj, t = divmod(i, VIEW_TILES)
+                piece = slice(i * P, (i + 1) * P)
+                nc.tensor.matmul_mx(
+                    out=lin_banks[c][t][:],
+                    lhsT=codes_now[:, piece].bitcast(FP8X4),
+                    lhsT_scale=scales_now[:, piece],
+                    rhs=w3_codes[:].bitcast(FP8X4),
+                    rhs_scale=w3_scales[:],
+                    start=(g == 0 and jj == 0),
+                    stop=(g == UNITS_PER_CHUNK - 1 and jj == UNIT_J - 1),
+                )
+
+        def linear_out_of_psum(c):
+            lin_rows[c] = chunk_pool.tile([P, VIEW_TILES, R], F32, name="lin_rows")
+            for t in range(VIEW_TILES):
+                nc.scalar.copy(out=lin_rows[c][:, t, :], in_=lin_banks[c][t][:])
+            folded[c] = chunk_pool.tile([P, R_BLOCKS, CHUNK_VIEWS], F32, name="folded")
+            nc.gpsimd.tensor_tensor(
+                out=folded[c][:],
+                in0=relu_sums[c][:, :, 0:CHUNK_VIEWS],
+                in1=relu_sums[c][:, :, CHUNK_VIEWS:BANK],
+                op=ALU.add,
+            )
+
+        def linear_transposes(c):
+            lin_cols[c] = []
+            for h in range(R_BLOCKS // 2):
+                lbank = psum_t.tile([P, 2, VIEW_TILES, P], F32, tag="t", name="lbank")
+                for s in range(2):
+                    m = 2 * h + s
+                    for t in range(VIEW_TILES):
+                        nc.tensor.transpose(lbank[:, s, t, :], lin_rows[c][:, t, m * P : (m + 1) * P], ident[:])
+                lin_cols[c].append(lbank)
+
+        def combine(c):
+            msum = chunk_pool.tile([P, R_BLOCKS, CHUNK_VIEWS], F32, name="msum")
+            for h in range(R_BLOCKS // 2):
+                nc.vector.scalar_tensor_tensor(
+                    out=msum[:, 2 * h : 2 * h + 2, :],
+                    in0=lin_cols[c][h][:].rearrange("p s t v -> p s (t v)"),
+                    scalar=LINEAR_OVER_RELU,
+                    in1=folded[c][:, 2 * h : 2 * h + 2, :],
+                    op0=ALU.mult,
+                    op1=ALU.add,
+                )
+            x_grouped[c] = chunk_pool.tile([P, CHUNK_VIEWS, PACK], BF16, align_bytes=64, name="x_grouped")
+            nc.scalar.mul(out=x_grouped[c][:], in_=msum[:].rearrange("p m v -> p v m"), mul=RELU_WEIGHT)
+
+        def fusion_layer(c):
+            x_codes = chunk_pool.tile([P, CHUNK_VIEWS], U32, align_bytes=64, name="x_codes")
+            x_scales = chunk_pool.tile([P, CHUNK_VIEWS], U8, align_bytes=64, name="x_scales")
+            quantise(x_grouped[c][:].rearrange("p v m -> p (v m)"), x_codes[:], x_scales[:])
+            for t in range(VIEW_TILES):
+                first = c * CHUNK_VIEWS + t * P
+                out_bank = psum_t.tile([P, O], F32, tag="t", name="out_bank")
+                nc.tensor.matmul_mx(
+                    out=out_bank[:],
+                    lhsT=feat_codes[:, first : first + P].bitcast(FP8X4),
+                    lhsT_scale=feat_scales[:, first : first + P],
+                    rhs=wf_codes[:, 0, :].bitcast(FP8X4),
+                    rhs_scale=wf_scales[:, 0, :],
+                    start=True,
+                    stop=False,
+                )
+                nc.tensor.matmul_mx(
+                    out=out_bank[:],
+                    lhsT=x_codes[:, t * P : (t + 1) * P].bitcast(FP8X4),
+                    lhsT_scale=x_scales[:, t * P : (t + 1) * P],
+                    rhs=wf_codes[:, 1, :].bitcast(FP8X4),
+                    rhs_scale=wf_scales[:, 1, :],
+                    start=False,
+                    stop=True,
+                )
+                result = store_pool.tile([P, O], F32, name="result")
+                nc.vector.tensor_tensor(out=result[:], in0=out_bank[:], in1=bf_all[:], op=ALU.add)
+                nc.sync.dma_start(out=out[first : first + P, :], in_=result[:])
+
+        for u in range(N_UNITS):
+            c, g = divmod(u, UNITS_PER_CHUNK)
+            if u + LOADS_AHEAD < N_UNITS:
+                raws[u + LOADS_AHEAD] = load_unit(u + LOADS_AHEAD)
+            if g == 0:
+                relu_sums[c] = chunk_pool.tile([P, R_BLOCKS, BANK], F32, name="relu_sums")
+                lin_banks[c] = []
+                for t in range(VIEW_TILES):
+                    lin_bank = psum_lin.tile([P, R], F32, tag="lin%d" % t, name="lin%d" % t)
+                    lin_banks[c].append(lin_bank)
+
+            if u + 1 < N_UNITS:
+                grouped_next = spread_k(raws[u + 1], unit_offsets)
+            if u == 1:
+                feat_grouped = spread_k(feat_raw, [t * WORDS for t in range(VIEWS // P)])
+            if g == 0 and c > 0:
+                linear_transposes(c - 1)
+
+            message_banks(u, 0, ROW_TILES // 2)
+            if u + 1 < N_UNITS:
+                codes_next, scales_next = quantise_unit(grouped_next)
+            if u == 1:
+                quantise(feat_grouped[:], feat_codes[:], feat_scales[:])
+            if g == 0 and c > 0:
+                combine(c - 1)
+            message_banks(u, ROW_TILES // 2, ROW_TILES)
+
+            if g == 1 and c > 0:
+                fusion_layer(c - 1)
+            if g == UNITS_PER_CHUNK - 1:
+                linear_out_of_psum(c)
+            if c == 0:
+                s, h = divmod(g, 2)
+                half = slice(h * (O // 2), (h + 1) * (O // 2))
+                nc.scalar.copy(
+                    out=wf_grouped[:, s, half, :], in_=wf_raw[:, s, :, half].rearrange("p t o -> p o t")
+                )
+                if g == UNITS_PER_CHUNK - 1:
+                    quantise(
+                        wf_grouped[:].rearrange("p s o t -> p (s o t)"),
+                        wf_codes[:].rearrange("p s o -> p (s o)"),
+                        wf_scales[:].rearrange("p s o -> p (s o)"),
+                    )
+            if u + 1 < N_UNITS:
+                codes_now, scales_now = codes_next, scales_next
+
+        linear_transposes(N_CHUNKS - 1)
+        combine(N_CHUNKS - 1)
+        fusion_layer(N_CHUNKS - 1)

@@ -9,6 +9,7 @@ U32 = mybir.dt.uint32
 U8 = mybir.dt.uint8
 FP8X4 = mybir.dt.float8_e4m3fn_x4
 ALU = mybir.AluOpType
+ACT = mybir.ActivationFunctionType
 
 P = 128
 PACK = 4
@@ -38,6 +39,7 @@ RELU_WEIGHT = 1.0 - NEG_SLOPE
 LINEAR_OVER_RELU = NEG_SLOPE / RELU_WEIGHT
 SEEDS = NEIGH + NEIGH * LINEAR_OVER_RELU
 HALVES = BANK // CHUNK_VIEWS
+VECTOR_BLOCKS = 3
 
 FLOPS = 2 * VIEWS * NEIGH * Q * R + 2 * VIEWS * (Q + R) * O
 
@@ -54,6 +56,7 @@ def tile_nonlocalmp_pb_kernel(tc, h2, feats, W3, b3, Wf, b_f, out):
         codes_pool = ctx.enter_context(tc.tile_pool(name="codes", bufs=2))
         chunk_pool = ctx.enter_context(tc.tile_pool(name="chunk", bufs=2))
         store_pool = ctx.enter_context(tc.tile_pool(name="store", bufs=3))
+        relu_pool = ctx.enter_context(tc.tile_pool(name="relu", bufs=3))
         psum_t = ctx.enter_context(tc.psum_pool(name="psum_t", bufs=3))
         psum_main = ctx.enter_context(tc.psum_pool(name="psum_main", bufs=3))
         psum_lin = ctx.enter_context(tc.psum_pool(name="psum_lin", bufs=1))
@@ -149,6 +152,10 @@ def tile_nonlocalmp_pb_kernel(tc, h2, feats, W3, b3, Wf, b_f, out):
         seed_b3 = consts.tile([P, R_BLOCKS], F32, name="seed_b3")
         nc.vector.tensor_scalar_mul(out=neg_b3[:], in0=b3_bank[:, 0:R_BLOCKS], scalar1=-1.0)
         nc.vector.tensor_scalar_mul(out=seed_b3[:], in0=b3_bank[:, 0:R_BLOCKS], scalar1=SEEDS / HALVES)
+        b3_cols = consts.tile([P, R_BLOCKS], F32, name="b3_cols")
+        late_b3 = consts.tile([P, R_BLOCKS], F32, name="late_b3")
+        nc.vector.tensor_copy(out=b3_cols[:], in_=b3_bank[:, 0:R_BLOCKS])
+        nc.vector.tensor_scalar_mul(out=late_b3[:], in0=b3_bank[:, 0:R_BLOCKS], scalar1=(SEEDS - NEIGH) / HALVES)
 
         feat_codes = consts.tile([P, VIEWS], U32, align_bytes=64, name="feat_codes")
         feat_scales = consts.tile([P, VIEWS], U8, align_bytes=64, name="feat_scales")
@@ -162,6 +169,7 @@ def tile_nonlocalmp_pb_kernel(tc, h2, feats, W3, b3, Wf, b_f, out):
         folded = {}
         lin_cols = {}
         x_grouped = {}
+        x_quantised = {}
 
         def message_banks(u, first, last):
             c, g = divmod(u, UNITS_PER_CHUNK)
@@ -180,7 +188,16 @@ def tile_nonlocalmp_pb_kernel(tc, h2, feats, W3, b3, Wf, b_f, out):
                     stop=True,
                 )
                 acc = relu_sums[c][:, m, :]
-                if g == 0 and jp == 0:
+                if m >= VECTOR_BLOCKS:
+                    relu = relu_pool.tile([P, BANK], F32, name="relu")
+                    nc.scalar.activation(out=relu[:], in_=main[:], func=ACT.Relu, bias=b3_cols[:, m : m + 1], scale=1.0)
+                    if g == 0 and jp == 0:
+                        nc.gpsimd.tensor_scalar(
+                            out=acc, in0=relu[:], scalar1=1.0, scalar2=late_b3[:, m : m + 1], op0=ALU.mult, op1=ALU.add
+                        )
+                    else:
+                        nc.gpsimd.tensor_tensor(out=acc, in0=relu[:], in1=acc, op=ALU.add)
+                elif g == 0 and jp == 0:
                     nc.vector.tensor_scalar(
                         out=acc,
                         in0=main[:],
@@ -212,68 +229,65 @@ def tile_nonlocalmp_pb_kernel(tc, h2, feats, W3, b3, Wf, b_f, out):
 
         def linear_out_of_psum(c):
             lin_rows[c] = chunk_pool.tile([P, VIEW_TILES, R], F32, name="lin_rows")
-            for t in range(VIEW_TILES):
-                nc.scalar.copy(out=lin_rows[c][:, t, :], in_=lin_banks[c][t][:])
             folded[c] = chunk_pool.tile([P, R_BLOCKS, CHUNK_VIEWS], F32, name="folded")
-            nc.gpsimd.tensor_tensor(
-                out=folded[c][:],
-                in0=relu_sums[c][:, :, 0:CHUNK_VIEWS],
-                in1=relu_sums[c][:, :, CHUNK_VIEWS:BANK],
-                op=ALU.add,
-            )
-
-        def linear_transposes(c):
-            lin_cols[c] = []
-            for h in range(R_BLOCKS // 2):
-                lbank = psum_t.tile([P, 2, VIEW_TILES, P], F32, tag="t", name="lbank")
-                for s in range(2):
-                    m = 2 * h + s
-                    for t in range(VIEW_TILES):
-                        nc.tensor.transpose(lbank[:, s, t, :], lin_rows[c][:, t, m * P : (m + 1) * P], ident[:])
-                lin_cols[c].append(lbank)
-
-        def combine(c):
-            msum = chunk_pool.tile([P, R_BLOCKS, CHUNK_VIEWS], F32, name="msum")
-            for h in range(R_BLOCKS // 2):
-                nc.vector.scalar_tensor_tensor(
-                    out=msum[:, 2 * h : 2 * h + 2, :],
-                    in0=lin_cols[c][h][:].rearrange("p s t v -> p s (t v)"),
-                    scalar=LINEAR_OVER_RELU,
-                    in1=folded[c][:, 2 * h : 2 * h + 2, :],
-                    op0=ALU.mult,
-                    op1=ALU.add,
-                )
-            x_grouped[c] = chunk_pool.tile([P, CHUNK_VIEWS, PACK], BF16, align_bytes=64, name="x_grouped")
-            nc.scalar.mul(out=x_grouped[c][:], in_=msum[:].rearrange("p m v -> p v m"), mul=RELU_WEIGHT)
-
-        def fusion_layer(c):
-            x_codes = chunk_pool.tile([P, CHUNK_VIEWS], U32, align_bytes=64, name="x_codes")
-            x_scales = chunk_pool.tile([P, CHUNK_VIEWS], U8, align_bytes=64, name="x_scales")
-            quantise(x_grouped[c][:].rearrange("p v m -> p (v m)"), x_codes[:], x_scales[:])
             for t in range(VIEW_TILES):
-                first = c * CHUNK_VIEWS + t * P
-                out_bank = psum_t.tile([P, O], F32, tag="t", name="out_bank")
-                nc.tensor.matmul_mx(
-                    out=out_bank[:],
-                    lhsT=feat_codes[:, first : first + P].bitcast(FP8X4),
-                    lhsT_scale=feat_scales[:, first : first + P],
-                    rhs=wf_codes[:, 0, :].bitcast(FP8X4),
-                    rhs_scale=wf_scales[:, 0, :],
-                    start=True,
-                    stop=False,
+                views = slice(t * P, (t + 1) * P)
+                later = slice(CHUNK_VIEWS + t * P, CHUNK_VIEWS + (t + 1) * P)
+                nc.scalar.copy(out=lin_rows[c][:, t, :], in_=lin_banks[c][t][:])
+                nc.gpsimd.tensor_tensor(
+                    out=folded[c][:, :, views], in0=relu_sums[c][:, :, views], in1=relu_sums[c][:, :, later], op=ALU.add
                 )
-                nc.tensor.matmul_mx(
-                    out=out_bank[:],
-                    lhsT=x_codes[:, t * P : (t + 1) * P].bitcast(FP8X4),
-                    lhsT_scale=x_scales[:, t * P : (t + 1) * P],
-                    rhs=wf_codes[:, 1, :].bitcast(FP8X4),
-                    rhs_scale=wf_scales[:, 1, :],
-                    start=False,
-                    stop=True,
-                )
-                result = store_pool.tile([P, O], F32, name="result")
-                nc.vector.tensor_tensor(out=result[:], in0=out_bank[:], in1=bf_all[:], op=ALU.add)
-                nc.sync.dma_start(out=out[first : first + P, :], in_=result[:])
+
+        def linear_transposes(c, t):
+            lbank = psum_t.tile([P, R_BLOCKS, P], F32, tag="t", name="lbank")
+            for m in range(R_BLOCKS):
+                nc.tensor.transpose(lbank[:, m, :], lin_rows[c][:, t, m * P : (m + 1) * P], ident[:])
+            lin_cols[c, t] = lbank
+
+        def combine(c, t):
+            msum = chunk_pool.tile([P, R_BLOCKS, P], F32, name="msum")
+            nc.vector.scalar_tensor_tensor(
+                out=msum[:],
+                in0=lin_cols[c, t][:],
+                scalar=LINEAR_OVER_RELU,
+                in1=folded[c][:, :, t * P : (t + 1) * P],
+                op0=ALU.mult,
+                op1=ALU.add,
+            )
+            x_grouped[c, t] = chunk_pool.tile([P, P, PACK], BF16, align_bytes=64, name="x_grouped")
+            nc.scalar.mul(out=x_grouped[c, t][:], in_=msum[:].rearrange("p m v -> p v m"), mul=RELU_WEIGHT)
+
+        def quantise_msum(c, t):
+            x_codes = chunk_pool.tile([P, P], U32, align_bytes=64, name="x_codes")
+            x_scales = chunk_pool.tile([P, P], U8, align_bytes=64, name="x_scales")
+            quantise(x_grouped[c, t][:].rearrange("p v m -> p (v m)"), x_codes[:], x_scales[:])
+            x_quantised[c, t] = (x_codes, x_scales)
+
+        def fusion_layer(c, t):
+            x_codes, x_scales = x_quantised[c, t]
+            first = c * CHUNK_VIEWS + t * P
+            out_bank = psum_t.tile([P, O], F32, tag="t", name="out_bank")
+            nc.tensor.matmul_mx(
+                out=out_bank[:],
+                lhsT=feat_codes[:, first : first + P].bitcast(FP8X4),
+                lhsT_scale=feat_scales[:, first : first + P],
+                rhs=wf_codes[:, 0, :].bitcast(FP8X4),
+                rhs_scale=wf_scales[:, 0, :],
+                start=True,
+                stop=False,
+            )
+            nc.tensor.matmul_mx(
+                out=out_bank[:],
+                lhsT=x_codes[:].bitcast(FP8X4),
+                lhsT_scale=x_scales[:],
+                rhs=wf_codes[:, 1, :].bitcast(FP8X4),
+                rhs_scale=wf_scales[:, 1, :],
+                start=False,
+                stop=True,
+            )
+            result = store_pool.tile([P, O], F32, name="result")
+            nc.vector.tensor_tensor(out=result[:], in0=out_bank[:], in1=bf_all[:], op=ALU.add)
+            nc.sync.dma_start(out=out[first : first + P, :], in_=result[:])
 
         for u in range(N_UNITS):
             c, g = divmod(u, UNITS_PER_CHUNK)
@@ -291,7 +305,8 @@ def tile_nonlocalmp_pb_kernel(tc, h2, feats, W3, b3, Wf, b_f, out):
             if u == 1:
                 feat_grouped = spread_k(feat_raw, [t * WORDS for t in range(VIEWS // P)])
             if g == 0 and c > 0:
-                linear_transposes(c - 1)
+                for t in range(VIEW_TILES):
+                    linear_transposes(c - 1, t)
 
             message_banks(u, 0, ROW_TILES // 2)
             if u + 1 < N_UNITS:
@@ -299,11 +314,15 @@ def tile_nonlocalmp_pb_kernel(tc, h2, feats, W3, b3, Wf, b_f, out):
             if u == 1:
                 quantise(feat_grouped[:], feat_codes[:], feat_scales[:])
             if g == 0 and c > 0:
-                combine(c - 1)
+                for t in range(VIEW_TILES):
+                    combine(c - 1, t)
             message_banks(u, ROW_TILES // 2, ROW_TILES)
 
             if g == 1 and c > 0:
-                fusion_layer(c - 1)
+                for t in range(VIEW_TILES):
+                    quantise_msum(c - 1, t)
+                for t in range(VIEW_TILES):
+                    fusion_layer(c - 1, t)
             if g == UNITS_PER_CHUNK - 1:
                 linear_out_of_psum(c)
             if c == 0:
@@ -321,6 +340,11 @@ def tile_nonlocalmp_pb_kernel(tc, h2, feats, W3, b3, Wf, b_f, out):
             if u + 1 < N_UNITS:
                 codes_now, scales_now = codes_next, scales_next
 
-        linear_transposes(N_CHUNKS - 1)
-        combine(N_CHUNKS - 1)
-        fusion_layer(N_CHUNKS - 1)
+        for t in range(VIEW_TILES):
+            linear_transposes(N_CHUNKS - 1, t)
+        for t in range(VIEW_TILES):
+            combine(N_CHUNKS - 1, t)
+        for t in range(VIEW_TILES):
+            quantise_msum(N_CHUNKS - 1, t)
+        for t in range(VIEW_TILES):
+            fusion_layer(N_CHUNKS - 1, t)

@@ -39,7 +39,9 @@ RELU_WEIGHT = 1.0 - NEG_SLOPE
 LINEAR_OVER_RELU = NEG_SLOPE / RELU_WEIGHT
 SEEDS = NEIGH + NEIGH * LINEAR_OVER_RELU
 HALVES = BANK // CHUNK_VIEWS
-VECTOR_BLOCKS = 3
+SCALAR_BLOCK = 1
+PAIRS = ROW_TILES // 2
+PAIR_COLS = 2 * P
 
 FLOPS = 2 * VIEWS * NEIGH * Q * R + 2 * VIEWS * (Q + R) * O
 
@@ -65,41 +67,46 @@ def tile_nonlocalmp_pb_kernel(tc, h2, feats, W3, b3, Wf, b_f, out):
         def load_unit(u):
             c, g = divmod(u, UNITS_PER_CHUNK)
             raw = raw_pool.tile([P, ROW_TILES * Q], BF16, name="raw")
-            rows = h2_rows[c * CHUNK_VIEWS : (c + 1) * CHUNK_VIEWS, g * UNIT_J : (g + 1) * UNIT_J, :]
-            nc.sync.dma_start(
-                out=raw[:].rearrange("p (t x) -> p t x", t=VIEW_TILES),
-                in_=rows.rearrange("(t p) j k -> p t (j k)", p=P),
-            )
+            raw_tiles = raw[:].rearrange("p (t x) -> p t x", t=VIEW_TILES)
+            views = slice(c * CHUNK_VIEWS, (c + 1) * CHUNK_VIEWS)
+            for hf in range(2):
+                first_j = g * UNIT_J + hf * (UNIT_J // 2)
+                nc.sync.dma_start(
+                    out=raw_tiles[:, :, hf * (UNIT_J // 2) * Q : (hf + 1) * (UNIT_J // 2) * Q],
+                    in_=h2_rows[views, first_j : first_j + UNIT_J // 2, :].rearrange("(t p) j k -> p t (j k)", p=P),
+                )
             return raw
 
-        def spread_k(raw, word_offsets):
+        def spread_pair(raw, word_offsets, grouped, pair):
             raw_words = raw[:].bitcast(F32)
-            grouped = grouped_pool.tile([P, UNIT_COLS * PACK], BF16, align_bytes=64, name="grouped")
             grouped_words = grouped[:].bitcast(F32).rearrange("p (c u) -> p c u", u=2)
-            for pair in range(ROW_TILES // 2):
-                bank = psum_t.tile([P, 2, 2, P], F32, tag="t", name="bank")
-                for s in range(2):
-                    for u in range(2):
-                        first = word_offsets[2 * pair + s] + u * P
-                        nc.tensor.transpose(bank[:, s, u, :], raw_words[:, first : first + P], ident[:])
-                nc.scalar.copy(
-                    out=grouped_words[:, 2 * pair * P : 2 * (pair + 1) * P, :].rearrange(
-                        "p (s r) u -> p s r u", s=2
-                    ),
-                    in_=bank[:].rearrange("p s u r -> p s r u"),
-                )
-            return grouped
+            bank = psum_t.tile([P, 2, 2, P], F32, tag="t", name="bank")
+            for s in range(2):
+                for u in range(2):
+                    first = word_offsets[2 * pair + s] + u * P
+                    nc.tensor.transpose(bank[:, s, u, :], raw_words[:, first : first + P], ident[:])
+            nc.scalar.copy(
+                out=grouped_words[:, pair * PAIR_COLS : (pair + 1) * PAIR_COLS, :].rearrange(
+                    "p (s r) u -> p s r u", s=2
+                ),
+                in_=bank[:].rearrange("p s u r -> p s r u"),
+            )
 
         def quantise(grouped_flat, codes_flat, scales_flat):
             nc.vector.quantize_mx(out=codes_flat.bitcast(FP8X4), scales=scales_flat, in_=grouped_flat)
 
-        def quantise_unit(grouped):
+        def quantise_pair(grouped, codes, scales, pair):
+            cols = slice(pair * PAIR_COLS, (pair + 1) * PAIR_COLS)
+            quantise(grouped[:, pair * PAIR_COLS * PACK : (pair + 1) * PAIR_COLS * PACK], codes[:, cols], scales[:, cols])
+
+        def new_unit_tiles():
+            grouped = grouped_pool.tile([P, UNIT_COLS * PACK], BF16, align_bytes=64, name="grouped")
             codes = codes_pool.tile([P, UNIT_COLS], U32, align_bytes=64, name="codes")
             scales = codes_pool.tile([P, UNIT_COLS], U8, align_bytes=64, name="scales")
-            quantise(grouped[:], codes[:], scales[:])
-            return codes, scales
+            return grouped, codes, scales
 
         unit_offsets = [(t * UNIT_J + jj) * WORDS for jj in range(UNIT_J) for t in range(VIEW_TILES)]
+        feat_offsets = [t * WORDS for t in range(VIEWS // P)]
 
         ident = consts.tile([P, P], F32, name="ident")
         make_identity(nc, ident[:])
@@ -133,7 +140,9 @@ def tile_nonlocalmp_pb_kernel(tc, h2, feats, W3, b3, Wf, b_f, out):
         nc.sync.dma_start(out=bf_all[:], in_=b_f.partition_broadcast(P))
         raws[3] = load_unit(3)
 
-        grouped_next = spread_k(raws[0], unit_offsets)
+        grouped_now, codes_now, scales_now = new_unit_tiles()
+        for pair in range(PAIRS):
+            spread_pair(raws[0], unit_offsets, grouped_now, pair)
 
         w3_grouped = consts.tile([P, R, PACK], BF16, align_bytes=64, name="w3_grouped")
         w3_codes = consts.tile([P, R], U32, align_bytes=64, name="w3_codes")
@@ -146,7 +155,8 @@ def tile_nonlocalmp_pb_kernel(tc, h2, feats, W3, b3, Wf, b_f, out):
         b3_bank = psum_t.tile([P, P], F32, tag="t", name="b3_bank")
         nc.tensor.transpose(b3_bank[:], b3_f32[:], ident[:])
 
-        codes_now, scales_now = quantise_unit(grouped_next)
+        for pair in range(PAIRS):
+            quantise_pair(grouped_now, codes_now, scales_now, pair)
 
         neg_b3 = consts.tile([P, R_BLOCKS], F32, name="neg_b3")
         seed_b3 = consts.tile([P, R_BLOCKS], F32, name="seed_b3")
@@ -157,6 +167,7 @@ def tile_nonlocalmp_pb_kernel(tc, h2, feats, W3, b3, Wf, b_f, out):
         nc.vector.tensor_copy(out=b3_cols[:], in_=b3_bank[:, 0:R_BLOCKS])
         nc.vector.tensor_scalar_mul(out=late_b3[:], in0=b3_bank[:, 0:R_BLOCKS], scalar1=(SEEDS - NEIGH) / HALVES)
 
+        feat_grouped = consts.tile([P, VIEWS * PACK], BF16, align_bytes=64, name="feat_grouped")
         feat_codes = consts.tile([P, VIEWS], U32, align_bytes=64, name="feat_codes")
         feat_scales = consts.tile([P, VIEWS], U8, align_bytes=64, name="feat_scales")
         wf_grouped = consts.tile([P, 2, O, PACK], BF16, align_bytes=64, name="wf_grouped")
@@ -171,61 +182,56 @@ def tile_nonlocalmp_pb_kernel(tc, h2, feats, W3, b3, Wf, b_f, out):
         x_grouped = {}
         x_quantised = {}
 
-        def message_banks(u, first, last):
+        def message_bank(u, i):
             c, g = divmod(u, UNITS_PER_CHUNK)
-            for i in range(first, last):
-                jp, m = divmod(i, R_BLOCKS)
-                block = slice(m * P, (m + 1) * P)
-                cols = slice(jp * BANK, (jp + 1) * BANK)
-                main = psum_main.tile([P, BANK], F32, name="main")
-                nc.tensor.matmul_mx(
-                    out=main[:],
-                    lhsT=w3_codes[:, block].bitcast(FP8X4),
-                    lhsT_scale=w3_scales[:, block],
-                    rhs=codes_now[:, cols].bitcast(FP8X4),
-                    rhs_scale=scales_now[:, cols],
-                    start=True,
-                    stop=True,
-                )
-                acc = relu_sums[c][:, m, :]
-                if m >= VECTOR_BLOCKS:
-                    relu = relu_pool.tile([P, BANK], F32, name="relu")
-                    nc.scalar.activation(out=relu[:], in_=main[:], func=ACT.Relu, bias=b3_cols[:, m : m + 1], scale=1.0)
-                    if g == 0 and jp == 0:
-                        nc.gpsimd.tensor_scalar(
-                            out=acc, in0=relu[:], scalar1=1.0, scalar2=late_b3[:, m : m + 1], op0=ALU.mult, op1=ALU.add
-                        )
-                    else:
-                        nc.gpsimd.tensor_tensor(out=acc, in0=relu[:], in1=acc, op=ALU.add)
-                elif g == 0 and jp == 0:
-                    nc.vector.tensor_scalar(
-                        out=acc,
-                        in0=main[:],
-                        scalar1=neg_b3[:, m : m + 1],
-                        scalar2=seed_b3[:, m : m + 1],
-                        op0=ALU.max,
-                        op1=ALU.add,
+            jp, m = divmod(i, R_BLOCKS)
+            block = slice(m * P, (m + 1) * P)
+            cols = slice(jp * BANK, (jp + 1) * BANK)
+            starts_chunk = g == 0 and jp == 0
+            main = psum_main.tile([P, BANK], F32, name="main")
+            nc.tensor.matmul_mx(
+                out=main[:],
+                lhsT=w3_codes[:, block].bitcast(FP8X4),
+                lhsT_scale=w3_scales[:, block],
+                rhs=codes_now[:, cols].bitcast(FP8X4),
+                rhs_scale=scales_now[:, cols],
+                start=True,
+                stop=True,
+            )
+            acc = relu_sums[c][:, m, :]
+            if m == SCALAR_BLOCK:
+                relu = relu_pool.tile([P, BANK], F32, name="relu")
+                nc.scalar.activation(out=relu[:], in_=main[:], func=ACT.Relu, bias=b3_cols[:, m : m + 1], scale=1.0)
+                if starts_chunk:
+                    nc.gpsimd.tensor_scalar(
+                        out=acc, in0=relu[:], scalar1=1.0, scalar2=late_b3[:, m : m + 1], op0=ALU.mult, op1=ALU.add
                     )
                 else:
-                    nc.vector.scalar_tensor_tensor(
-                        out=acc,
-                        in0=main[:],
-                        scalar=neg_b3[:, m : m + 1],
-                        in1=acc,
-                        op0=ALU.max,
-                        op1=ALU.add,
-                    )
-                jj, t = divmod(i, VIEW_TILES)
-                piece = slice(i * P, (i + 1) * P)
-                nc.tensor.matmul_mx(
-                    out=lin_banks[c][t][:],
-                    lhsT=codes_now[:, piece].bitcast(FP8X4),
-                    lhsT_scale=scales_now[:, piece],
-                    rhs=w3_codes[:].bitcast(FP8X4),
-                    rhs_scale=w3_scales[:],
-                    start=(g == 0 and jj == 0),
-                    stop=(g == UNITS_PER_CHUNK - 1 and jj == UNIT_J - 1),
+                    nc.gpsimd.tensor_tensor(out=acc, in0=relu[:], in1=acc, op=ALU.add)
+            elif starts_chunk:
+                nc.vector.tensor_scalar(
+                    out=acc,
+                    in0=main[:],
+                    scalar1=neg_b3[:, m : m + 1],
+                    scalar2=seed_b3[:, m : m + 1],
+                    op0=ALU.max,
+                    op1=ALU.add,
                 )
+            else:
+                nc.vector.scalar_tensor_tensor(
+                    out=acc, in0=main[:], scalar=neg_b3[:, m : m + 1], in1=acc, op0=ALU.max, op1=ALU.add
+                )
+            jj, t = divmod(i, VIEW_TILES)
+            piece = slice(i * P, (i + 1) * P)
+            nc.tensor.matmul_mx(
+                out=lin_banks[c][t][:],
+                lhsT=codes_now[:, piece].bitcast(FP8X4),
+                lhsT_scale=scales_now[:, piece],
+                rhs=w3_codes[:].bitcast(FP8X4),
+                rhs_scale=w3_scales[:],
+                start=(g == 0 and jj == 0),
+                stop=(g == UNITS_PER_CHUNK - 1 and jj == UNIT_J - 1),
+            )
 
         def linear_out_of_psum(c):
             lin_rows[c] = chunk_pool.tile([P, VIEW_TILES, R], F32, name="lin_rows")
@@ -291,6 +297,7 @@ def tile_nonlocalmp_pb_kernel(tc, h2, feats, W3, b3, Wf, b_f, out):
 
         for u in range(N_UNITS):
             c, g = divmod(u, UNITS_PER_CHUNK)
+            more = u + 1 < N_UNITS
             if u + LOADS_AHEAD < N_UNITS:
                 raws[u + LOADS_AHEAD] = load_unit(u + LOADS_AHEAD)
             if g == 0:
@@ -300,36 +307,32 @@ def tile_nonlocalmp_pb_kernel(tc, h2, feats, W3, b3, Wf, b_f, out):
                     lin_bank = psum_lin.tile([P, R], F32, tag="lin%d" % t, name="lin%d" % t)
                     lin_banks[c].append(lin_bank)
 
-            if u + 1 < N_UNITS:
-                grouped_next = spread_k(raws[u + 1], unit_offsets)
-            if u == 1:
-                feat_grouped = spread_k(feat_raw, [t * WORDS for t in range(VIEWS // P)])
-            if g == 0 and c > 0:
-                for t in range(VIEW_TILES):
-                    linear_transposes(c - 1, t)
-
-            message_banks(u, 0, ROW_TILES // 2)
-            if u + 1 < N_UNITS:
-                codes_next, scales_next = quantise_unit(grouped_next)
-            if u == 1:
-                quantise(feat_grouped[:], feat_codes[:], feat_scales[:])
-            if g == 0 and c > 0:
-                for t in range(VIEW_TILES):
-                    combine(c - 1, t)
-            message_banks(u, ROW_TILES // 2, ROW_TILES)
-
-            if g == 1 and c > 0:
-                for t in range(VIEW_TILES):
-                    quantise_msum(c - 1, t)
-                for t in range(VIEW_TILES):
-                    fusion_layer(c - 1, t)
-            if g == UNITS_PER_CHUNK - 1:
-                linear_out_of_psum(c)
+            if more:
+                grouped_next, codes_next, scales_next = new_unit_tiles()
+                for pair in range(PAIRS):
+                    spread_pair(raws[u + 1], unit_offsets, grouped_next, pair)
             if c == 0:
+                spread_pair(feat_raw, feat_offsets, feat_grouped, g)
+            if c > 0 and g < VIEW_TILES:
+                linear_transposes(c - 1, g)
+                combine(c - 1, g)
+
+            for i in range(ROW_TILES):
+                message_bank(u, i)
+                if more and i % 2 == 1:
+                    quantise_pair(grouped_next, codes_next, scales_next, i // 2)
+
+            if c == 0:
+                quantise_pair(feat_grouped, feat_codes, feat_scales, g)
                 s, h = divmod(g, 2)
                 half = slice(h * (O // 2), (h + 1) * (O // 2))
-                nc.scalar.copy(
-                    out=wf_grouped[:, s, half, :], in_=wf_raw[:, s, :, half].rearrange("p t o -> p o t")
+                nc.gpsimd.tensor_scalar(
+                    out=wf_grouped[:, s, half, :],
+                    in0=wf_raw[:, s, :, half].rearrange("p t o -> p o t"),
+                    scalar1=1.0,
+                    scalar2=0.0,
+                    op0=ALU.mult,
+                    op1=ALU.add,
                 )
                 if g == UNITS_PER_CHUNK - 1:
                     quantise(
@@ -337,7 +340,12 @@ def tile_nonlocalmp_pb_kernel(tc, h2, feats, W3, b3, Wf, b_f, out):
                         wf_codes[:].rearrange("p s o -> p (s o)"),
                         wf_scales[:].rearrange("p s o -> p (s o)"),
                     )
-            if u + 1 < N_UNITS:
+            if c > 0 and g >= VIEW_TILES:
+                quantise_msum(c - 1, g - VIEW_TILES)
+                fusion_layer(c - 1, g - VIEW_TILES)
+            if g == UNITS_PER_CHUNK - 1:
+                linear_out_of_psum(c)
+            if more:
                 codes_now, scales_now = codes_next, scales_next
 
         for t in range(VIEW_TILES):

@@ -33,13 +33,17 @@ ROW_TILES = VIEW_TILES * UNIT_J
 UNIT_COLS = ROW_TILES * P
 R_BLOCKS = R // P
 BANK = 512
-LOADS_AHEAD = 4
+LOADS_AHEAD = 6
+AHEAD = 2
 
 RELU_WEIGHT = 1.0 - NEG_SLOPE
 LINEAR_OVER_RELU = NEG_SLOPE / RELU_WEIGHT
 SEEDS = NEIGH + NEIGH * LINEAR_OVER_RELU
 HALVES = BANK // CHUNK_VIEWS
 SCALAR_BLOCK = 1
+SCALAR_NEIGH = NEIGH // 2
+BANKS = [(0, m) for m in range(R_BLOCKS)] + [(1, m) for m in range(R_BLOCKS) if m != SCALAR_BLOCK] + [(1, SCALAR_BLOCK)]
+SCALAR_BANK = (0, SCALAR_BLOCK)
 PAIRS = ROW_TILES // 2
 PAIR_COLS = 2 * P
 
@@ -55,7 +59,7 @@ def tile_nonlocalmp_pb_kernel(tc, h2, feats, W3, b3, Wf, b_f, out):
         consts = ctx.enter_context(tc.tile_pool(name="consts", bufs=1))
         raw_pool = ctx.enter_context(tc.tile_pool(name="raw", bufs=LOADS_AHEAD + 1))
         grouped_pool = ctx.enter_context(tc.tile_pool(name="grouped", bufs=3))
-        codes_pool = ctx.enter_context(tc.tile_pool(name="codes", bufs=2))
+        codes_pool = ctx.enter_context(tc.tile_pool(name="codes", bufs=3))
         chunk_pool = ctx.enter_context(tc.tile_pool(name="chunk", bufs=2))
         store_pool = ctx.enter_context(tc.tile_pool(name="store", bufs=3))
         relu_pool = ctx.enter_context(tc.tile_pool(name="relu", bufs=3))
@@ -95,9 +99,9 @@ def tile_nonlocalmp_pb_kernel(tc, h2, feats, W3, b3, Wf, b_f, out):
         def quantise(grouped_flat, codes_flat, scales_flat):
             nc.vector.quantize_mx(out=codes_flat.bitcast(FP8X4), scales=scales_flat, in_=grouped_flat)
 
-        def quantise_pair(grouped, codes, scales, pair):
-            cols = slice(pair * PAIR_COLS, (pair + 1) * PAIR_COLS)
-            quantise(grouped[:, pair * PAIR_COLS * PACK : (pair + 1) * PAIR_COLS * PACK], codes[:, cols], scales[:, cols])
+        def quantise_cols(grouped, codes, scales, first, width):
+            cols = slice(first, first + width)
+            quantise(grouped[:, first * PACK : (first + width) * PACK], codes[:, cols], scales[:, cols])
 
         def new_unit_tiles():
             grouped = grouped_pool.tile([P, UNIT_COLS * PACK], BF16, align_bytes=64, name="grouped")
@@ -112,14 +116,13 @@ def tile_nonlocalmp_pb_kernel(tc, h2, feats, W3, b3, Wf, b_f, out):
         make_identity(nc, ident[:])
         b3_rows = consts.tile([P, P], BF16, name="b3_rows")
         nc.vector.memset(b3_rows[:], 0.0)
-
-        raws = {0: load_unit(0)}
+        nc.sync.dma_start(out=b3_rows[0:R_BLOCKS, :], in_=b3.rearrange("(m p) -> m p", p=P))
         w3_raw = consts.tile([P, PACK, R], BF16, name="w3_raw")
         nc.sync.dma_start(
             out=w3_raw[:].rearrange("p (u e) r -> p u (e r)", e=2),
             in_=W3.rearrange("(u q e) r -> q u (e r)", u=2, e=2),
         )
-        nc.sync.dma_start(out=b3_rows[0:R_BLOCKS, :], in_=b3.rearrange("(m p) -> m p", p=P))
+        raws = {0: load_unit(0)}
         raws[1] = load_unit(1)
         raws[2] = load_unit(2)
         feat_raw = consts.tile([P, (VIEWS // P) * Q], BF16, name="feat_raw")
@@ -127,6 +130,7 @@ def tile_nonlocalmp_pb_kernel(tc, h2, feats, W3, b3, Wf, b_f, out):
             out=feat_raw[:].rearrange("p (t k) -> p t k", k=Q),
             in_=feat_rows.rearrange("(t p) k -> p t k", p=P),
         )
+        raws[3] = load_unit(3)
         wf_raw = consts.tile([P, 2, PACK, O], BF16, name="wf_raw")
         nc.sync.dma_start(
             out=wf_raw[:, 0, :, :].rearrange("p (u e) o -> p u (e o)", e=2),
@@ -136,36 +140,42 @@ def tile_nonlocalmp_pb_kernel(tc, h2, feats, W3, b3, Wf, b_f, out):
             out=wf_raw[:, 1, :, :],
             in_=Wf[K_PASS : 2 * K_PASS, :].rearrange("(t p) o -> p t o", p=P),
         )
+        raws[4] = load_unit(4)
+        raws[5] = load_unit(5)
         bf_all = consts.tile([P, O], BF16, name="bf_all")
         nc.sync.dma_start(out=bf_all[:], in_=b_f.partition_broadcast(P))
-        raws[3] = load_unit(3)
-
-        grouped_now, codes_now, scales_now = new_unit_tiles()
-        for pair in range(PAIRS):
-            spread_pair(raws[0], unit_offsets, grouped_now, pair)
-
-        w3_grouped = consts.tile([P, R, PACK], BF16, align_bytes=64, name="w3_grouped")
-        w3_codes = consts.tile([P, R], U32, align_bytes=64, name="w3_codes")
-        w3_scales = consts.tile([P, R], U8, align_bytes=64, name="w3_scales")
-        nc.vector.tensor_copy(out=w3_grouped[:], in_=w3_raw[:].rearrange("p t r -> p r t"))
-        quantise(w3_grouped[:].rearrange("p r t -> p (r t)"), w3_codes[:], w3_scales[:])
 
         b3_f32 = consts.tile([P, P], F32, name="b3_f32")
         nc.vector.tensor_copy(out=b3_f32[:], in_=b3_rows[:])
         b3_bank = psum_t.tile([P, P], F32, tag="t", name="b3_bank")
         nc.tensor.transpose(b3_bank[:], b3_f32[:], ident[:])
 
+        tiles = {0: new_unit_tiles()}
         for pair in range(PAIRS):
-            quantise_pair(grouped_now, codes_now, scales_now, pair)
+            spread_pair(raws[0], unit_offsets, tiles[0][0], pair)
+        tiles[1] = new_unit_tiles()
+        for pair in range(PAIRS):
+            spread_pair(raws[1], unit_offsets, tiles[1][0], pair)
+
+        w3_grouped = consts.tile([P, R, PACK], BF16, align_bytes=64, name="w3_grouped")
+        w3_codes = consts.tile([P, R], U32, align_bytes=64, name="w3_codes")
+        w3_scales = consts.tile([P, R], U8, align_bytes=64, name="w3_scales")
+        for h in range(2):
+            half = slice(h * (R // 2), (h + 1) * (R // 2))
+            nc.vector.tensor_copy(out=w3_grouped[:, half, :], in_=w3_raw[:, :, half].rearrange("p t r -> p r t"))
+        b3_cols = consts.tile([P, R_BLOCKS], F32, name="b3_cols")
+        nc.vector.tensor_copy(out=b3_cols[:], in_=b3_bank[:, 0:R_BLOCKS])
+        quantise(w3_grouped[:].rearrange("p r t -> p (r t)"), w3_codes[:], w3_scales[:])
 
         neg_b3 = consts.tile([P, R_BLOCKS], F32, name="neg_b3")
         seed_b3 = consts.tile([P, R_BLOCKS], F32, name="seed_b3")
-        nc.vector.tensor_scalar_mul(out=neg_b3[:], in0=b3_bank[:, 0:R_BLOCKS], scalar1=-1.0)
-        nc.vector.tensor_scalar_mul(out=seed_b3[:], in0=b3_bank[:, 0:R_BLOCKS], scalar1=SEEDS / HALVES)
-        b3_cols = consts.tile([P, R_BLOCKS], F32, name="b3_cols")
         late_b3 = consts.tile([P, R_BLOCKS], F32, name="late_b3")
-        nc.vector.tensor_copy(out=b3_cols[:], in_=b3_bank[:, 0:R_BLOCKS])
-        nc.vector.tensor_scalar_mul(out=late_b3[:], in0=b3_bank[:, 0:R_BLOCKS], scalar1=(SEEDS - NEIGH) / HALVES)
+        nc.vector.tensor_scalar_mul(out=neg_b3[:], in0=b3_cols[:], scalar1=-1.0)
+        nc.vector.tensor_scalar_mul(out=seed_b3[:], in0=b3_cols[:], scalar1=SEEDS / HALVES)
+        nc.vector.tensor_scalar_mul(out=late_b3[:], in0=b3_cols[:], scalar1=(SEEDS - SCALAR_NEIGH) / HALVES)
+
+        for pair in range(PAIRS):
+            quantise_cols(*tiles[0], pair * PAIR_COLS, PAIR_COLS)
 
         feat_grouped = consts.tile([P, VIEWS * PACK], BF16, align_bytes=64, name="feat_grouped")
         feat_codes = consts.tile([P, VIEWS], U32, align_bytes=64, name="feat_codes")
@@ -184,7 +194,8 @@ def tile_nonlocalmp_pb_kernel(tc, h2, feats, W3, b3, Wf, b_f, out):
 
         def message_bank(u, i):
             c, g = divmod(u, UNITS_PER_CHUNK)
-            jp, m = divmod(i, R_BLOCKS)
+            jp, m = BANKS[i]
+            codes_now, scales_now = tiles[u][1:]
             block = slice(m * P, (m + 1) * P)
             cols = slice(jp * BANK, (jp + 1) * BANK)
             starts_chunk = g == 0 and jp == 0
@@ -199,7 +210,7 @@ def tile_nonlocalmp_pb_kernel(tc, h2, feats, W3, b3, Wf, b_f, out):
                 stop=True,
             )
             acc = relu_sums[c][:, m, :]
-            if m == SCALAR_BLOCK:
+            if (jp, m) == SCALAR_BANK:
                 relu = relu_pool.tile([P, BANK], F32, name="relu")
                 nc.scalar.activation(out=relu[:], in_=main[:], func=ACT.Relu, bias=b3_cols[:, m : m + 1], scale=1.0)
                 if starts_chunk:
@@ -233,16 +244,15 @@ def tile_nonlocalmp_pb_kernel(tc, h2, feats, W3, b3, Wf, b_f, out):
                 stop=(g == UNITS_PER_CHUNK - 1 and jj == UNIT_J - 1),
             )
 
-        def linear_out_of_psum(c):
-            lin_rows[c] = chunk_pool.tile([P, VIEW_TILES, R], F32, name="lin_rows")
-            folded[c] = chunk_pool.tile([P, R_BLOCKS, CHUNK_VIEWS], F32, name="folded")
-            for t in range(VIEW_TILES):
-                views = slice(t * P, (t + 1) * P)
-                later = slice(CHUNK_VIEWS + t * P, CHUNK_VIEWS + (t + 1) * P)
-                nc.scalar.copy(out=lin_rows[c][:, t, :], in_=lin_banks[c][t][:])
-                nc.gpsimd.tensor_tensor(
-                    out=folded[c][:, :, views], in0=relu_sums[c][:, :, views], in1=relu_sums[c][:, :, later], op=ALU.add
-                )
+        def linear_out_of_psum(c, t, copy):
+            copy(out=lin_rows[c][:, t, :], in_=lin_banks[c][t][:])
+
+        def fold(c, t):
+            views = slice(t * P, (t + 1) * P)
+            later = slice(CHUNK_VIEWS + t * P, CHUNK_VIEWS + (t + 1) * P)
+            nc.gpsimd.tensor_tensor(
+                out=folded[c][:, :, views], in0=relu_sums[c][:, :, views], in1=relu_sums[c][:, :, later], op=ALU.add
+            )
 
         def linear_transposes(c, t):
             lbank = psum_t.tile([P, R_BLOCKS, P], F32, tag="t", name="lbank")
@@ -297,58 +307,67 @@ def tile_nonlocalmp_pb_kernel(tc, h2, feats, W3, b3, Wf, b_f, out):
 
         for u in range(N_UNITS):
             c, g = divmod(u, UNITS_PER_CHUNK)
-            more = u + 1 < N_UNITS
             if u + LOADS_AHEAD < N_UNITS:
                 raws[u + LOADS_AHEAD] = load_unit(u + LOADS_AHEAD)
             if g == 0:
                 relu_sums[c] = chunk_pool.tile([P, R_BLOCKS, BANK], F32, name="relu_sums")
+                lin_rows[c] = chunk_pool.tile([P, VIEW_TILES, R], F32, name="lin_rows")
+                folded[c] = chunk_pool.tile([P, R_BLOCKS, CHUNK_VIEWS], F32, name="folded")
                 lin_banks[c] = []
                 for t in range(VIEW_TILES):
                     lin_bank = psum_lin.tile([P, R], F32, tag="lin%d" % t, name="lin%d" % t)
                     lin_banks[c].append(lin_bank)
-
-            if more:
-                grouped_next, codes_next, scales_next = new_unit_tiles()
-                for pair in range(PAIRS):
-                    spread_pair(raws[u + 1], unit_offsets, grouped_next, pair)
-            if c == 0:
-                spread_pair(feat_raw, feat_offsets, feat_grouped, g)
-            if c > 0 and g < VIEW_TILES:
-                linear_transposes(c - 1, g)
-                combine(c - 1, g)
+            finishing = c > 0
 
             for i in range(ROW_TILES):
                 message_bank(u, i)
-                if more and i % 2 == 1:
-                    quantise_pair(grouped_next, codes_next, scales_next, i // 2)
-
-            if c == 0:
-                quantise_pair(feat_grouped, feat_codes, feat_scales, g)
-                s, h = divmod(g, 2)
-                half = slice(h * (O // 2), (h + 1) * (O // 2))
-                nc.gpsimd.tensor_scalar(
-                    out=wf_grouped[:, s, half, :],
-                    in0=wf_raw[:, s, :, half].rearrange("p t o -> p o t"),
-                    scalar1=1.0,
-                    scalar2=0.0,
-                    op0=ALU.mult,
-                    op1=ALU.add,
-                )
-                if g == UNITS_PER_CHUNK - 1:
-                    quantise(
-                        wf_grouped[:].rearrange("p s o t -> p (s o t)"),
-                        wf_codes[:].rearrange("p s o -> p (s o)"),
-                        wf_scales[:].rearrange("p s o -> p (s o)"),
+                if i == 1 and finishing and g < VIEW_TILES:
+                    fold(c - 1, g)
+                if i == 3 and 1 <= u <= 4:
+                    s, h = divmod(u - 1, 2)
+                    half = slice(h * (O // 2), (h + 1) * (O // 2))
+                    nc.gpsimd.tensor_scalar(
+                        out=wf_grouped[:, s, half, :],
+                        in0=wf_raw[:, s, :, half].rearrange("p t o -> p o t"),
+                        scalar1=1.0,
+                        scalar2=0.0,
+                        op0=ALU.mult,
+                        op1=ALU.add,
                     )
-            if c > 0 and g >= VIEW_TILES:
-                quantise_msum(c - 1, g - VIEW_TILES)
-                fusion_layer(c - 1, g - VIEW_TILES)
+
             if g == UNITS_PER_CHUNK - 1:
-                linear_out_of_psum(c)
-            if more:
-                codes_now, scales_now = codes_next, scales_next
+                linear_out_of_psum(c, 0, nc.scalar.copy)
+            if u + AHEAD < N_UNITS:
+                tiles[u + AHEAD] = new_unit_tiles()
+                for pair in range(PAIRS):
+                    spread_pair(raws[u + AHEAD], unit_offsets, tiles[u + AHEAD][0], pair)
+            if c == 0:
+                spread_pair(feat_raw, feat_offsets, feat_grouped, g)
+            if finishing and g < VIEW_TILES:
+                linear_transposes(c - 1, g)
+
+            if u + 1 < N_UNITS:
+                quantise_cols(*tiles[u + 1], 0, BANK)
+            if g == UNITS_PER_CHUNK - 1:
+                linear_out_of_psum(c, 1, nc.vector.tensor_copy)
+            if u + 1 < N_UNITS:
+                quantise_cols(*tiles[u + 1], BANK, BANK)
+
+            if 1 <= u <= UNITS_PER_CHUNK:
+                quantise_cols(feat_grouped, feat_codes, feat_scales, (u - 1) * PAIR_COLS, PAIR_COLS)
+            if u == 3 or u == 5:
+                s = (u - 3) // 2
+                quantise(wf_grouped[:, s, :, :].rearrange("p o t -> p (o t)"), wf_codes[:, s, :], wf_scales[:, s, :])
+            if finishing:
+                if 0 < g <= VIEW_TILES:
+                    quantise_msum(c - 1, g - 1)
+                if g < VIEW_TILES:
+                    combine(c - 1, g)
+                if g >= 2:
+                    fusion_layer(c - 1, g - 2)
 
         for t in range(VIEW_TILES):
+            fold(N_CHUNKS - 1, t)
             linear_transposes(N_CHUNKS - 1, t)
         for t in range(VIEW_TILES):
             combine(N_CHUNKS - 1, t)

@@ -63,8 +63,7 @@ def tile_nonlocalmp_pb_kernel(tc, h2, feats, W3, b3, Wf, b_f, out):
         chunk_pool = ctx.enter_context(tc.tile_pool(name="chunk", bufs=2))
         store_pool = ctx.enter_context(tc.tile_pool(name="store", bufs=3))
         relu_pool = ctx.enter_context(tc.tile_pool(name="relu", bufs=3))
-        psum_t = ctx.enter_context(tc.psum_pool(name="psum_t", bufs=3))
-        psum_main = ctx.enter_context(tc.psum_pool(name="psum_main", bufs=3))
+        psum_ring = ctx.enter_context(tc.psum_pool(name="psum_ring", bufs=6))
         psum_lin = ctx.enter_context(tc.psum_pool(name="psum_lin", bufs=1))
         ctx.enter_context(tc.manual_schedule())
 
@@ -84,7 +83,7 @@ def tile_nonlocalmp_pb_kernel(tc, h2, feats, W3, b3, Wf, b_f, out):
         def spread_pair(raw, word_offsets, grouped, pair):
             raw_words = raw[:].bitcast(F32)
             grouped_words = grouped[:].bitcast(F32).rearrange("p (c u) -> p c u", u=2)
-            bank = psum_t.tile([P, 2, 2, P], F32, tag="t", name="bank")
+            bank = psum_ring.tile([P, 2, 2, P], F32, tag="ring", name="bank")
             for s in range(2):
                 for u in range(2):
                     first = word_offsets[2 * pair + s] + u * P
@@ -147,7 +146,7 @@ def tile_nonlocalmp_pb_kernel(tc, h2, feats, W3, b3, Wf, b_f, out):
 
         b3_f32 = consts.tile([P, P], F32, name="b3_f32")
         nc.vector.tensor_copy(out=b3_f32[:], in_=b3_rows[:])
-        b3_bank = psum_t.tile([P, P], F32, tag="t", name="b3_bank")
+        b3_bank = psum_ring.tile([P, P], F32, tag="ring", name="b3_bank")
         nc.tensor.transpose(b3_bank[:], b3_f32[:], ident[:])
 
         tiles = {0: new_unit_tiles()}
@@ -199,7 +198,7 @@ def tile_nonlocalmp_pb_kernel(tc, h2, feats, W3, b3, Wf, b_f, out):
             block = slice(m * P, (m + 1) * P)
             cols = slice(jp * BANK, (jp + 1) * BANK)
             starts_chunk = g == 0 and jp == 0
-            main = psum_main.tile([P, BANK], F32, name="main")
+            main = psum_ring.tile([P, BANK], F32, tag="ring", name="main")
             nc.tensor.matmul_mx(
                 out=main[:],
                 lhsT=w3_codes[:, block].bitcast(FP8X4),
@@ -255,7 +254,7 @@ def tile_nonlocalmp_pb_kernel(tc, h2, feats, W3, b3, Wf, b_f, out):
             )
 
         def linear_transposes(c, t):
-            lbank = psum_t.tile([P, R_BLOCKS, P], F32, tag="t", name="lbank")
+            lbank = psum_ring.tile([P, R_BLOCKS, P], F32, tag="ring", name="lbank")
             for m in range(R_BLOCKS):
                 nc.tensor.transpose(lbank[:, m, :], lin_rows[c][:, t, m * P : (m + 1) * P], ident[:])
             lin_cols[c, t] = lbank
@@ -282,7 +281,7 @@ def tile_nonlocalmp_pb_kernel(tc, h2, feats, W3, b3, Wf, b_f, out):
         def fusion_layer(c, t):
             x_codes, x_scales = x_quantised[c, t]
             first = c * CHUNK_VIEWS + t * P
-            out_bank = psum_t.tile([P, O], F32, tag="t", name="out_bank")
+            out_bank = psum_ring.tile([P, O], F32, tag="ring", name="out_bank")
             nc.tensor.matmul_mx(
                 out=out_bank[:],
                 lhsT=feat_codes[:, first : first + P].bitcast(FP8X4),

@@ -27,6 +27,7 @@ VIEW_TILES = 2
 CHUNK_VIEWS = VIEW_TILES * P
 N_CHUNKS = VIEWS // CHUNK_VIEWS
 UNIT_J = 4
+HALF_J = UNIT_J // 2
 UNITS_PER_CHUNK = NEIGH // UNIT_J
 N_UNITS = N_CHUNKS * UNITS_PER_CHUNK
 ROW_TILES = VIEW_TILES * UNIT_J
@@ -34,6 +35,12 @@ UNIT_COLS = ROW_TILES * P
 R_BLOCKS = R // P
 BANK = 512
 LOADS_AHEAD = 6
+FT = {1:[0],2:[1],3:[2,3]}
+WFQ = [(1, 6), (2, 3), (3, 3), (4, 3)]
+TA = {0:[2],1:[4],2:[5],3:[6],4:[7],5:[8],6:[9],7:[10],8:[11],9:[12],10:[13],11:[14],12:[15]}
+TM = {0:[1],1:[3]}
+QA = {0:[1],1:[2],2:[3,4],3:[5],4:[6],5:[7],6:[8],7:[9],8:[10],9:[11],10:[12],11:[13],12:[14],13:[15]}
+LAST = N_UNITS - 1
 AHEAD = 2
 
 RELU_WEIGHT = 1.0 - NEG_SLOPE
@@ -58,8 +65,8 @@ def tile_nonlocalmp_pb_kernel(tc, h2, feats, W3, b3, Wf, b_f, out):
     with ExitStack() as ctx:
         consts = ctx.enter_context(tc.tile_pool(name="consts", bufs=1))
         raw_pool = ctx.enter_context(tc.tile_pool(name="raw", bufs=LOADS_AHEAD + 1))
-        grouped_pool = ctx.enter_context(tc.tile_pool(name="grouped", bufs=3))
-        codes_pool = ctx.enter_context(tc.tile_pool(name="codes", bufs=3))
+        grouped_pool = ctx.enter_context(tc.tile_pool(name="grouped", bufs=4))
+        codes_pool = ctx.enter_context(tc.tile_pool(name="codes", bufs=4))
         chunk_pool = ctx.enter_context(tc.tile_pool(name="chunk", bufs=2))
         store_pool = ctx.enter_context(tc.tile_pool(name="store", bufs=3))
         relu_pool = ctx.enter_context(tc.tile_pool(name="relu", bufs=3))
@@ -67,26 +74,29 @@ def tile_nonlocalmp_pb_kernel(tc, h2, feats, W3, b3, Wf, b_f, out):
         psum_lin = ctx.enter_context(tc.psum_pool(name="psum_lin", bufs=1))
         ctx.enter_context(tc.manual_schedule())
 
-        def load_unit(u):
+        def load_unit(u, between=None):
             c, g = divmod(u, UNITS_PER_CHUNK)
-            raw = raw_pool.tile([P, ROW_TILES * Q], BF16, name="raw")
-            raw_tiles = raw[:].rearrange("p (t x) -> p t x", t=VIEW_TILES)
             views = slice(c * CHUNK_VIEWS, (c + 1) * CHUNK_VIEWS)
+            halves = []
             for hf in range(2):
-                first_j = g * UNIT_J + hf * (UNIT_J // 2)
+                raw = raw_pool.tile([P, VIEW_TILES, HALF_J * Q], BF16, tag="raw%d" % hf, name="raw")
+                first_j = g * UNIT_J + hf * HALF_J
                 nc.sync.dma_start(
-                    out=raw_tiles[:, :, hf * (UNIT_J // 2) * Q : (hf + 1) * (UNIT_J // 2) * Q],
-                    in_=h2_rows[views, first_j : first_j + UNIT_J // 2, :].rearrange("(t p) j k -> p t (j k)", p=P),
+                    out=raw[:],
+                    in_=h2_rows[views, first_j : first_j + HALF_J, :].rearrange("(t p) j k -> p t (j k)", p=P),
                 )
-            return raw
+                halves.append(raw[:].rearrange("p t x -> p (t x)"))
+                if between is not None and hf == 0:
+                    between()
+            return halves
 
         def spread_pair(raw, word_offsets, grouped, pair):
-            raw_words = raw[:].bitcast(F32)
+            raw_words = raw.bitcast(F32)
             grouped_words = grouped[:].bitcast(F32).rearrange("p (c u) -> p c u", u=2)
             bank = psum_ring.tile([P, 2, 2, P], F32, tag="ring", name="bank")
             for s in range(2):
                 for u in range(2):
-                    first = word_offsets[2 * pair + s] + u * P
+                    first = word_offsets[s] + u * P
                     nc.tensor.transpose(bank[:, s, u, :], raw_words[:, first : first + P], ident[:])
             nc.scalar.copy(
                 out=grouped_words[:, pair * PAIR_COLS : (pair + 1) * PAIR_COLS, :].rearrange(
@@ -108,28 +118,32 @@ def tile_nonlocalmp_pb_kernel(tc, h2, feats, W3, b3, Wf, b_f, out):
             scales = codes_pool.tile([P, UNIT_COLS], U8, align_bytes=64, name="scales")
             return grouped, codes, scales
 
-        unit_offsets = [(t * UNIT_J + jj) * WORDS for jj in range(UNIT_J) for t in range(VIEW_TILES)]
-        feat_offsets = [t * WORDS for t in range(VIEWS // P)]
+        unit_offsets = [[(t * HALF_J + jj) * WORDS for t in range(VIEW_TILES)] for jj in range(HALF_J)]
+        feat_offsets = [[t * WORDS, (t + 1) * WORDS] for t in range(0, VIEWS // P, 2)]
 
         ident = consts.tile([P, P], F32, name="ident")
         make_identity(nc, ident[:])
+        w3_raw = consts.tile([P, PACK, R], BF16, name="w3_raw")
+
+        def load_w3():
+            nc.sync.dma_start(
+                out=w3_raw[:].rearrange("p (u e) r -> p u (e r)", e=2),
+                in_=W3.rearrange("(u q e) r -> q u (e r)", u=2, e=2),
+            )
+
+        raws = {0: load_unit(0, load_w3)}
         b3_rows = consts.tile([P, P], BF16, name="b3_rows")
         nc.vector.memset(b3_rows[:], 0.0)
         nc.sync.dma_start(out=b3_rows[0:R_BLOCKS, :], in_=b3.rearrange("(m p) -> m p", p=P))
-        w3_raw = consts.tile([P, PACK, R], BF16, name="w3_raw")
-        nc.sync.dma_start(
-            out=w3_raw[:].rearrange("p (u e) r -> p u (e r)", e=2),
-            in_=W3.rearrange("(u q e) r -> q u (e r)", u=2, e=2),
-        )
-        raws = {0: load_unit(0)}
         raws[1] = load_unit(1)
         raws[2] = load_unit(2)
-        feat_raw = consts.tile([P, (VIEWS // P) * Q], BF16, name="feat_raw")
+        raws[3] = load_unit(3)
+        raws[4] = load_unit(4)
+        feat_raw = consts.tile([P, VIEWS // P, Q], BF16, name="feat_raw")
         nc.sync.dma_start(
-            out=feat_raw[:].rearrange("p (t k) -> p t k", k=Q),
+            out=feat_raw[:],
             in_=feat_rows.rearrange("(t p) k -> p t k", p=P),
         )
-        raws[3] = load_unit(3)
         wf_raw = consts.tile([P, 2, PACK, O], BF16, name="wf_raw")
         nc.sync.dma_start(
             out=wf_raw[:, 0, :, :].rearrange("p (u e) o -> p u (e o)", e=2),
@@ -139,22 +153,13 @@ def tile_nonlocalmp_pb_kernel(tc, h2, feats, W3, b3, Wf, b_f, out):
             out=wf_raw[:, 1, :, :],
             in_=Wf[K_PASS : 2 * K_PASS, :].rearrange("(t p) o -> p t o", p=P),
         )
-        raws[4] = load_unit(4)
         raws[5] = load_unit(5)
         bf_all = consts.tile([P, O], BF16, name="bf_all")
         nc.sync.dma_start(out=bf_all[:], in_=b_f.partition_broadcast(P))
 
-        b3_f32 = consts.tile([P, P], F32, name="b3_f32")
-        nc.vector.tensor_copy(out=b3_f32[:], in_=b3_rows[:])
-        b3_bank = psum_ring.tile([P, P], F32, tag="ring", name="b3_bank")
-        nc.tensor.transpose(b3_bank[:], b3_f32[:], ident[:])
-
         tiles = {0: new_unit_tiles()}
         for pair in range(PAIRS):
-            spread_pair(raws[0], unit_offsets, tiles[0][0], pair)
-        tiles[1] = new_unit_tiles()
-        for pair in range(PAIRS):
-            spread_pair(raws[1], unit_offsets, tiles[1][0], pair)
+            spread_pair(raws[0][pair // HALF_J], unit_offsets[pair % HALF_J], tiles[0][0], pair)
 
         w3_grouped = consts.tile([P, R, PACK], BF16, align_bytes=64, name="w3_grouped")
         w3_codes = consts.tile([P, R], U32, align_bytes=64, name="w3_codes")
@@ -162,18 +167,23 @@ def tile_nonlocalmp_pb_kernel(tc, h2, feats, W3, b3, Wf, b_f, out):
         for h in range(2):
             half = slice(h * (R // 2), (h + 1) * (R // 2))
             nc.vector.tensor_copy(out=w3_grouped[:, half, :], in_=w3_raw[:, :, half].rearrange("p t r -> p r t"))
-        b3_cols = consts.tile([P, R_BLOCKS], F32, name="b3_cols")
-        nc.vector.tensor_copy(out=b3_cols[:], in_=b3_bank[:, 0:R_BLOCKS])
+        quantise_cols(*tiles[0], 0, PAIR_COLS)
+        b3_f32 = consts.tile([P, P], F32, name="b3_f32")
+        nc.vector.tensor_copy(out=b3_f32[:], in_=b3_rows[:])
+        b3_bank = psum_ring.tile([P, P], F32, tag="ring", name="b3_bank")
+        nc.tensor.transpose(b3_bank[:], b3_f32[:], ident[:])
         quantise(w3_grouped[:].rearrange("p r t -> p (r t)"), w3_codes[:], w3_scales[:])
+        quantise_cols(*tiles[0], PAIR_COLS, PAIR_COLS)
 
+        b3_cols = consts.tile([P, R_BLOCKS], F32, name="b3_cols")
         neg_b3 = consts.tile([P, R_BLOCKS], F32, name="neg_b3")
         seed_b3 = consts.tile([P, R_BLOCKS], F32, name="seed_b3")
         late_b3 = consts.tile([P, R_BLOCKS], F32, name="late_b3")
+        nc.vector.tensor_copy(out=b3_cols[:], in_=b3_bank[:, 0:R_BLOCKS])
         nc.vector.tensor_scalar_mul(out=neg_b3[:], in0=b3_cols[:], scalar1=-1.0)
         nc.vector.tensor_scalar_mul(out=seed_b3[:], in0=b3_cols[:], scalar1=SEEDS / HALVES)
         nc.vector.tensor_scalar_mul(out=late_b3[:], in0=b3_cols[:], scalar1=(SEEDS - SCALAR_NEIGH) / HALVES)
-
-        for pair in range(PAIRS):
+        for pair in range(PAIRS // 2, PAIRS):
             quantise_cols(*tiles[0], pair * PAIR_COLS, PAIR_COLS)
 
         feat_grouped = consts.tile([P, VIEWS * PACK], BF16, align_bytes=64, name="feat_grouped")
@@ -184,12 +194,28 @@ def tile_nonlocalmp_pb_kernel(tc, h2, feats, W3, b3, Wf, b_f, out):
         wf_scales = consts.tile([P, 2, O], U8, align_bytes=64, name="wf_scales")
 
         relu_sums = {}
+        waiting = []
         lin_banks = {}
         lin_rows = {}
         folded = {}
         lin_cols = {}
         x_grouped = {}
         x_quantised = {}
+
+        def linear_pass(u, i):
+            c, g = divmod(u, UNITS_PER_CHUNK)
+            codes, scales = tiles[u][1:]
+            jj, t = divmod(i, VIEW_TILES)
+            piece = slice(i * P, (i + 1) * P)
+            nc.tensor.matmul_mx(
+                out=lin_banks[c][t][:],
+                lhsT=codes[:, piece].bitcast(FP8X4),
+                lhsT_scale=scales[:, piece],
+                rhs=w3_codes[:].bitcast(FP8X4),
+                rhs_scale=w3_scales[:],
+                start=(g == 0 and jj == 0),
+                stop=(g == UNITS_PER_CHUNK - 1 and jj == UNIT_J - 1),
+            )
 
         def message_bank(u, i):
             c, g = divmod(u, UNITS_PER_CHUNK)
@@ -213,9 +239,8 @@ def tile_nonlocalmp_pb_kernel(tc, h2, feats, W3, b3, Wf, b_f, out):
                 relu = relu_pool.tile([P, BANK], F32, name="relu")
                 nc.scalar.activation(out=relu[:], in_=main[:], func=ACT.Relu, bias=b3_cols[:, m : m + 1], scale=1.0)
                 if starts_chunk:
-                    nc.gpsimd.tensor_scalar(
-                        out=acc, in0=relu[:], scalar1=1.0, scalar2=late_b3[:, m : m + 1], op0=ALU.mult, op1=ALU.add
-                    )
+                    seed = late_b3[:, m : m + 1]
+                    nc.gpsimd.tensor_scalar(out=acc, in0=relu[:], scalar1=1.0, scalar2=seed, op0=ALU.mult, op1=ALU.add)
                 else:
                     nc.gpsimd.tensor_tensor(out=acc, in0=relu[:], in1=acc, op=ALU.add)
             elif starts_chunk:
@@ -231,26 +256,15 @@ def tile_nonlocalmp_pb_kernel(tc, h2, feats, W3, b3, Wf, b_f, out):
                 nc.vector.scalar_tensor_tensor(
                     out=acc, in0=main[:], scalar=neg_b3[:, m : m + 1], in1=acc, op0=ALU.max, op1=ALU.add
                 )
-            jj, t = divmod(i, VIEW_TILES)
-            piece = slice(i * P, (i + 1) * P)
-            nc.tensor.matmul_mx(
-                out=lin_banks[c][t][:],
-                lhsT=codes_now[:, piece].bitcast(FP8X4),
-                lhsT_scale=scales_now[:, piece],
-                rhs=w3_codes[:].bitcast(FP8X4),
-                rhs_scale=w3_scales[:],
-                start=(g == 0 and jj == 0),
-                stop=(g == UNITS_PER_CHUNK - 1 and jj == UNIT_J - 1),
-            )
-
-        def linear_out_of_psum(c, t, copy):
-            copy(out=lin_rows[c][:, t, :], in_=lin_banks[c][t][:])
+        def linear_out_of_psum(c, t):
+            nc.scalar.copy(out=lin_rows[c][:, t, :], in_=lin_banks[c][t][:])
 
         def fold(c, t):
             views = slice(t * P, (t + 1) * P)
             later = slice(CHUNK_VIEWS + t * P, CHUNK_VIEWS + (t + 1) * P)
+            folded[c, t] = chunk_pool.tile([P, R_BLOCKS, P], F32, tag="folded%d" % t, name="folded")
             nc.gpsimd.tensor_tensor(
-                out=folded[c][:, :, views], in0=relu_sums[c][:, :, views], in1=relu_sums[c][:, :, later], op=ALU.add
+                out=folded[c, t][:], in0=relu_sums[c][:, :, views], in1=relu_sums[c][:, :, later], op=ALU.add
             )
 
         def linear_transposes(c, t):
@@ -259,18 +273,25 @@ def tile_nonlocalmp_pb_kernel(tc, h2, feats, W3, b3, Wf, b_f, out):
                 nc.tensor.transpose(lbank[:, m, :], lin_rows[c][:, t, m * P : (m + 1) * P], ident[:])
             lin_cols[c, t] = lbank
 
-        def combine(c, t):
+        def new_x(c, t):
+            x_grouped[c, t] = chunk_pool.tile([P, P, PACK], BF16, align_bytes=64, name="x_grouped")
+            return x_grouped[c, t]
+
+        def add_linear(c, t):
             msum = chunk_pool.tile([P, R_BLOCKS, P], F32, name="msum")
             nc.vector.scalar_tensor_tensor(
                 out=msum[:],
                 in0=lin_cols[c, t][:],
                 scalar=LINEAR_OVER_RELU,
-                in1=folded[c][:, :, t * P : (t + 1) * P],
+                in1=folded[c, t][:],
                 op0=ALU.mult,
                 op1=ALU.add,
             )
-            x_grouped[c, t] = chunk_pool.tile([P, P, PACK], BF16, align_bytes=64, name="x_grouped")
-            nc.scalar.mul(out=x_grouped[c, t][:], in_=msum[:].rearrange("p m v -> p v m"), mul=RELU_WEIGHT)
+            return msum
+
+        def combine(c, t):
+            msum = add_linear(c, t)
+            nc.scalar.mul(out=new_x(c, t)[:], in_=msum[:].rearrange("p m v -> p v m"), mul=RELU_WEIGHT)
 
         def quantise_msum(c, t):
             x_codes = chunk_pool.tile([P, P], U32, align_bytes=64, name="x_codes")
@@ -278,8 +299,7 @@ def tile_nonlocalmp_pb_kernel(tc, h2, feats, W3, b3, Wf, b_f, out):
             quantise(x_grouped[c, t][:].rearrange("p v m -> p (v m)"), x_codes[:], x_scales[:])
             x_quantised[c, t] = (x_codes, x_scales)
 
-        def fusion_layer(c, t):
-            x_codes, x_scales = x_quantised[c, t]
+        def fusion_feats(c, t):
             first = c * CHUNK_VIEWS + t * P
             out_bank = psum_ring.tile([P, O], F32, tag="ring", name="out_bank")
             nc.tensor.matmul_mx(
@@ -291,6 +311,10 @@ def tile_nonlocalmp_pb_kernel(tc, h2, feats, W3, b3, Wf, b_f, out):
                 start=True,
                 stop=False,
             )
+            return out_bank
+
+        def fusion_msum(c, t, out_bank):
+            x_codes, x_scales = x_quantised[c, t]
             nc.tensor.matmul_mx(
                 out=out_bank[:],
                 lhsT=x_codes[:].bitcast(FP8X4),
@@ -300,18 +324,22 @@ def tile_nonlocalmp_pb_kernel(tc, h2, feats, W3, b3, Wf, b_f, out):
                 start=False,
                 stop=True,
             )
-            result = store_pool.tile([P, O], F32, name="result")
-            nc.vector.tensor_tensor(out=result[:], in0=out_bank[:], in1=bf_all[:], op=ALU.add)
-            nc.sync.dma_start(out=out[first : first + P, :], in_=result[:])
 
-        for u in range(N_UNITS):
+        def store_out(c, t, out_bank, pieces):
+            first = c * CHUNK_VIEWS + t * P
+            for k in range(pieces):
+                cols = slice(k * O // pieces, (k + 1) * O // pieces)
+                result = store_pool.tile([P, O // pieces], F32, tag="result%d" % pieces, name="result")
+                nc.vector.tensor_tensor(out=result[:], in0=out_bank[:, cols], in1=bf_all[:, cols], op=ALU.add)
+                nc.sync.dma_start(out=out[first : first + P, cols], in_=result[:])
+
+        for u in range(LAST):
             c, g = divmod(u, UNITS_PER_CHUNK)
             if u + LOADS_AHEAD < N_UNITS:
                 raws[u + LOADS_AHEAD] = load_unit(u + LOADS_AHEAD)
             if g == 0:
                 relu_sums[c] = chunk_pool.tile([P, R_BLOCKS, BANK], F32, name="relu_sums")
                 lin_rows[c] = chunk_pool.tile([P, VIEW_TILES, R], F32, name="lin_rows")
-                folded[c] = chunk_pool.tile([P, R_BLOCKS, CHUNK_VIEWS], F32, name="folded")
                 lin_banks[c] = []
                 for t in range(VIEW_TILES):
                     lin_bank = psum_lin.tile([P, R], F32, tag="lin%d" % t, name="lin%d" % t)
@@ -320,57 +348,93 @@ def tile_nonlocalmp_pb_kernel(tc, h2, feats, W3, b3, Wf, b_f, out):
 
             for i in range(ROW_TILES):
                 message_bank(u, i)
-                if i == 1 and finishing and g < VIEW_TILES:
-                    fold(c - 1, g)
-                if i == 3 and 1 <= u <= 4:
-                    s, h = divmod(u - 1, 2)
+                linear_pass(u, i)
+                if i == 1 and waiting:
+                    store_out(*waiting.pop(), 1)
+                if i == R_BLOCKS - 1:
+                    for w in TM.get(u, ()):
+                        tiles[w] = new_unit_tiles()
+                        for pair in range(PAIRS):
+                            spread_pair(raws[w][pair // HALF_J], unit_offsets[pair % HALF_J], tiles[w][0], pair)
+                if i == 1 and finishing and g == 0:
+                    for t in range(VIEW_TILES):
+                        fold(c - 1, t)
+                if i == 5 and finishing and g == 1:
+                    for t in range(VIEW_TILES):
+                        quantise_msum(c - 1, t)
+                if (u, i) in WFQ:
+                    s, h = divmod(WFQ.index((u, i)), 2)
                     half = slice(h * (O // 2), (h + 1) * (O // 2))
-                    nc.gpsimd.tensor_scalar(
-                        out=wf_grouped[:, s, half, :],
-                        in0=wf_raw[:, s, :, half].rearrange("p t o -> p o t"),
-                        scalar1=1.0,
-                        scalar2=0.0,
-                        op0=ALU.mult,
-                        op1=ALU.add,
+                    nc.scalar.copy(
+                        out=wf_grouped[:, s, half, :], in_=wf_raw[:, s, :, half].rearrange("p t o -> p o t")
                     )
 
-            if g == UNITS_PER_CHUNK - 1:
-                linear_out_of_psum(c, 0, nc.scalar.copy)
-            if u + AHEAD < N_UNITS:
-                tiles[u + AHEAD] = new_unit_tiles()
+            ends_chunk = g == UNITS_PER_CHUNK - 1
+            if ends_chunk:
+                linear_out_of_psum(c, 0)
+            for w in TA.get(u, ()):
+                tiles[w] = new_unit_tiles()
                 for pair in range(PAIRS):
-                    spread_pair(raws[u + AHEAD], unit_offsets, tiles[u + AHEAD][0], pair)
-            if c == 0:
-                spread_pair(feat_raw, feat_offsets, feat_grouped, g)
-            if finishing and g < VIEW_TILES:
-                linear_transposes(c - 1, g)
+                    spread_pair(raws[w][pair // HALF_J], unit_offsets[pair % HALF_J], tiles[w][0], pair)
+                    if ends_chunk and pair == 1:
+                        linear_out_of_psum(c, 1)
+            for k in FT.get(u, ()):
+                spread_pair(feat_raw[:].rearrange("p t k -> p (t k)"), feat_offsets[k], feat_grouped, k)
+            if finishing and g == 0:
+                for t in range(VIEW_TILES):
+                    linear_transposes(c - 1, t)
 
-            if u + 1 < N_UNITS:
-                quantise_cols(*tiles[u + 1], 0, BANK)
-            if g == UNITS_PER_CHUNK - 1:
-                linear_out_of_psum(c, 1, nc.vector.tensor_copy)
-            if u + 1 < N_UNITS:
-                quantise_cols(*tiles[u + 1], BANK, BANK)
+            for w in QA.get(u, ()):
+                for h in range(HALVES):
+                    quantise_cols(*tiles[w], h * BANK, BANK)
 
-            if 1 <= u <= UNITS_PER_CHUNK:
-                quantise_cols(feat_grouped, feat_codes, feat_scales, (u - 1) * PAIR_COLS, PAIR_COLS)
-            if u == 3 or u == 5:
-                s = (u - 3) // 2
+            for k in FT.get(u - 1, ()):
+                quantise_cols(feat_grouped, feat_codes, feat_scales, k * PAIR_COLS, PAIR_COLS)
+            if u == 3 or u == 4:
+                s = u - 3
                 quantise(wf_grouped[:, s, :, :].rearrange("p o t -> p (o t)"), wf_codes[:, s, :], wf_scales[:, s, :])
             if finishing:
+                if g == 0:
+                    for t in range(VIEW_TILES):
+                        combine(c - 1, t)
                 if 0 < g <= VIEW_TILES:
-                    quantise_msum(c - 1, g - 1)
-                if g < VIEW_TILES:
-                    combine(c - 1, g)
-                if g >= 2:
-                    fusion_layer(c - 1, g - 2)
+                    out_bank = fusion_feats(c - 1, g - 1)
+                    fusion_msum(c - 1, g - 1, out_bank)
+                    waiting.append((c - 1, g - 1, out_bank))
 
+        c = N_CHUNKS - 1
+        for i in range(ROW_TILES - 2):
+            message_bank(LAST, i)
+            linear_pass(LAST, i)
+            if i == 1:
+                store_out(*waiting.pop(), 1)
+        for i in range(ROW_TILES - 2, ROW_TILES):
+            linear_pass(LAST, i)
         for t in range(VIEW_TILES):
-            fold(N_CHUNKS - 1, t)
-            linear_transposes(N_CHUNKS - 1, t)
+            linear_out_of_psum(c, t)
+        for i in range(ROW_TILES - 2, ROW_TILES):
+            message_bank(LAST, i)
+        out_banks = []
         for t in range(VIEW_TILES):
-            combine(N_CHUNKS - 1, t)
-        for t in range(VIEW_TILES):
-            quantise_msum(N_CHUNKS - 1, t)
-        for t in range(VIEW_TILES):
-            fusion_layer(N_CHUNKS - 1, t)
+            out_banks.append(fusion_feats(c, t))
+        for t in reversed(range(VIEW_TILES)):
+            linear_transposes(c, t)
+        fold(c, 0)
+        folded[c, 1] = chunk_pool.tile([P, R_BLOCKS, P], F32, tag="folded1", name="folded")
+        nc.vector.tensor_tensor(
+            out=folded[c, 1][:],
+            in0=relu_sums[c][:, :, P : 2 * P],
+            in1=relu_sums[c][:, :, CHUNK_VIEWS + P : CHUNK_VIEWS + 2 * P],
+            op=ALU.add,
+        )
+        combine(c, 1)
+        msum = add_linear(c, 0)
+        x_rows = new_x(c, 0)
+        by_view = msum[:].rearrange("p m v -> p v m")
+        nc.scalar.mul(out=x_rows[:, 0 : P // 2, :], in_=by_view[:, 0 : P // 2, :], mul=RELU_WEIGHT)
+        nc.vector.tensor_scalar_mul(out=x_rows[:, P // 2 : P, :], in0=by_view[:, P // 2 : P, :], scalar1=RELU_WEIGHT)
+        for t in reversed(range(VIEW_TILES)):
+            quantise_msum(c, t)
+            fusion_msum(c, t, out_banks[t])
+        for t in reversed(range(VIEW_TILES)):
+            store_out(c, t, out_banks[t], 2 - t)

@@ -69,7 +69,7 @@ def tile_nonlocalmp_pb_kernel(tc, h2, feats, W3, b3, Wf, b_f, out):
         codes_pool = ctx.enter_context(tc.tile_pool(name="codes", bufs=4))
         chunk_pool = ctx.enter_context(tc.tile_pool(name="chunk", bufs=2))
         store_pool = ctx.enter_context(tc.tile_pool(name="store", bufs=3))
-        relu_pool = ctx.enter_context(tc.tile_pool(name="relu", bufs=3))
+        relu_pool = ctx.enter_context(tc.tile_pool(name="relu", bufs=4))
         psum_ring = ctx.enter_context(tc.psum_pool(name="psum_ring", bufs=6))
         psum_lin = ctx.enter_context(tc.psum_pool(name="psum_lin", bufs=1))
         ctx.enter_context(tc.manual_schedule())
@@ -181,8 +181,8 @@ def tile_nonlocalmp_pb_kernel(tc, h2, feats, W3, b3, Wf, b_f, out):
         late_b3 = consts.tile([P, R_BLOCKS], F32, name="late_b3")
         nc.vector.tensor_copy(out=b3_cols[:], in_=b3_bank[:, 0:R_BLOCKS])
         nc.vector.tensor_scalar_mul(out=neg_b3[:], in0=b3_cols[:], scalar1=-1.0)
-        nc.vector.tensor_scalar_mul(out=seed_b3[:], in0=b3_cols[:], scalar1=SEEDS / HALVES)
-        nc.vector.tensor_scalar_mul(out=late_b3[:], in0=b3_cols[:], scalar1=(SEEDS - SCALAR_NEIGH) / HALVES)
+        nc.vector.tensor_scalar_mul(out=seed_b3[:], in0=b3_cols[:], scalar1=SEEDS - HALVES)
+        nc.vector.tensor_scalar_mul(out=late_b3[:], in0=b3_cols[:], scalar1=SEEDS - SCALAR_NEIGH)
         for pair in range(PAIRS // 2, PAIRS):
             quantise_cols(*tiles[0], pair * PAIR_COLS, PAIR_COLS)
 
@@ -194,6 +194,7 @@ def tile_nonlocalmp_pb_kernel(tc, h2, feats, W3, b3, Wf, b_f, out):
         wf_scales = consts.tile([P, 2, O], U8, align_bytes=64, name="wf_scales")
 
         relu_sums = {}
+        starts = {}
         waiting = []
         lin_banks = {}
         lin_rows = {}
@@ -235,37 +236,33 @@ def tile_nonlocalmp_pb_kernel(tc, h2, feats, W3, b3, Wf, b_f, out):
                 stop=True,
             )
             acc = relu_sums[c][:, m, :]
-            if (jp, m) == SCALAR_BANK:
+            if starts_chunk:
+                starts[c, m] = relu_pool.tile([P, BANK], F32, tag="start", name="start")
+                nc.scalar.activation(out=starts[c, m][:], in_=main[:], func=ACT.Relu, bias=b3_cols[:, m : m + 1], scale=1.0)
+            elif (jp, m) == SCALAR_BANK:
                 relu = relu_pool.tile([P, BANK], F32, name="relu")
                 nc.scalar.activation(out=relu[:], in_=main[:], func=ACT.Relu, bias=b3_cols[:, m : m + 1], scale=1.0)
-                if starts_chunk:
-                    seed = late_b3[:, m : m + 1]
-                    nc.gpsimd.tensor_scalar(out=acc, in0=relu[:], scalar1=1.0, scalar2=seed, op0=ALU.mult, op1=ALU.add)
-                else:
-                    nc.gpsimd.tensor_tensor(out=acc, in0=relu[:], in1=acc, op=ALU.add)
-            elif starts_chunk:
-                nc.vector.tensor_scalar(
-                    out=acc,
-                    in0=main[:],
-                    scalar1=neg_b3[:, m : m + 1],
-                    scalar2=seed_b3[:, m : m + 1],
-                    op0=ALU.max,
-                    op1=ALU.add,
-                )
+                nc.gpsimd.tensor_tensor(out=acc, in0=relu[:], in1=acc, op=ALU.add)
             else:
+                before = starts[c, m][:] if g == 0 and jp == 1 else acc
                 nc.vector.scalar_tensor_tensor(
-                    out=acc, in0=main[:], scalar=neg_b3[:, m : m + 1], in1=acc, op0=ALU.max, op1=ALU.add
+                    out=acc, in0=main[:], scalar=neg_b3[:, m : m + 1], in1=before, op0=ALU.max, op1=ALU.add
                 )
         def linear_out_of_psum(c, t):
             nc.scalar.copy(out=lin_rows[c][:, t, :], in_=lin_banks[c][t][:])
 
-        def fold(c, t):
-            views = slice(t * P, (t + 1) * P)
-            later = slice(CHUNK_VIEWS + t * P, CHUNK_VIEWS + (t + 1) * P)
-            folded[c, t] = chunk_pool.tile([P, R_BLOCKS, P], F32, tag="folded%d" % t, name="folded")
-            nc.gpsimd.tensor_tensor(
-                out=folded[c, t][:], in0=relu_sums[c][:, :, views], in1=relu_sums[c][:, :, later], op=ALU.add
-            )
+        def fold(c):
+            folded[c] = chunk_pool.tile([P, R_BLOCKS, CHUNK_VIEWS], F32, name="folded")
+            for m in range(R_BLOCKS):
+                sums = relu_sums[c][:, m, :]
+                nc.vector.scalar_tensor_tensor(
+                    out=folded[c][:, m, :],
+                    in0=sums[:, 0:CHUNK_VIEWS],
+                    scalar=(late_b3 if m == SCALAR_BLOCK else seed_b3)[:, m : m + 1],
+                    in1=sums[:, CHUNK_VIEWS : 2 * CHUNK_VIEWS],
+                    op0=ALU.add,
+                    op1=ALU.add,
+                )
 
         def linear_transposes(c, t):
             lbank = psum_ring.tile([P, R_BLOCKS, P], F32, tag="ring", name="lbank")
@@ -283,7 +280,7 @@ def tile_nonlocalmp_pb_kernel(tc, h2, feats, W3, b3, Wf, b_f, out):
                 out=msum[:],
                 in0=lin_cols[c, t][:],
                 scalar=LINEAR_OVER_RELU,
-                in1=folded[c, t][:],
+                in1=folded[c][:, :, t * P : (t + 1) * P],
                 op0=ALU.mult,
                 op1=ALU.add,
             )
@@ -356,9 +353,8 @@ def tile_nonlocalmp_pb_kernel(tc, h2, feats, W3, b3, Wf, b_f, out):
                         tiles[w] = new_unit_tiles()
                         for pair in range(PAIRS):
                             spread_pair(raws[w][pair // HALF_J], unit_offsets[pair % HALF_J], tiles[w][0], pair)
-                if i == 1 and finishing and g == 0:
-                    for t in range(VIEW_TILES):
-                        fold(c - 1, t)
+                if i == 3 and finishing and g == 0:
+                    fold(c - 1)
                 if i == 5 and finishing and g == 1:
                     for t in range(VIEW_TILES):
                         quantise_msum(c - 1, t)
@@ -419,14 +415,7 @@ def tile_nonlocalmp_pb_kernel(tc, h2, feats, W3, b3, Wf, b_f, out):
             out_banks.append(fusion_feats(c, t))
         for t in reversed(range(VIEW_TILES)):
             linear_transposes(c, t)
-        fold(c, 0)
-        folded[c, 1] = chunk_pool.tile([P, R_BLOCKS, P], F32, tag="folded1", name="folded")
-        nc.vector.tensor_tensor(
-            out=folded[c, 1][:],
-            in0=relu_sums[c][:, :, P : 2 * P],
-            in1=relu_sums[c][:, :, CHUNK_VIEWS + P : CHUNK_VIEWS + 2 * P],
-            op=ALU.add,
-        )
+        fold(c)
         combine(c, 1)
         msum = add_linear(c, 0)
         x_rows = new_x(c, 0)

@@ -114,8 +114,8 @@ def tile_nonlocalmp_pb_kernel(tc, h2, feats, W3, b3, Wf, b_f, out):
 
         def new_unit_tiles():
             grouped = grouped_pool.tile([P, UNIT_COLS * PACK], BF16, align_bytes=64, name="grouped")
-            codes = codes_pool.tile([P, UNIT_COLS], U32, align_bytes=64, name="codes")
-            scales = codes_pool.tile([P, UNIT_COLS], U8, align_bytes=64, name="scales")
+            codes = codes_pool.tile([P, UNIT_COLS], U32, align_bytes=256, name="codes")
+            scales = codes_pool.tile([P, UNIT_COLS], U8, align_bytes=256, name="scales")
             return grouped, codes, scales
 
         unit_offsets = [[(t * HALF_J + jj) * WORDS for t in range(VIEW_TILES)] for jj in range(HALF_J)]
@@ -162,8 +162,8 @@ def tile_nonlocalmp_pb_kernel(tc, h2, feats, W3, b3, Wf, b_f, out):
             spread_pair(raws[0][pair // HALF_J], unit_offsets[pair % HALF_J], tiles[0][0], pair)
 
         w3_grouped = consts.tile([P, R, PACK], BF16, align_bytes=64, name="w3_grouped")
-        w3_codes = consts.tile([P, R], U32, align_bytes=64, name="w3_codes")
-        w3_scales = consts.tile([P, R], U8, align_bytes=64, name="w3_scales")
+        w3_codes = consts.tile([P, R], U32, align_bytes=256, name="w3_codes")
+        w3_scales = consts.tile([P, R], U8, align_bytes=256, name="w3_scales")
         for h in range(2):
             half = slice(h * (R // 2), (h + 1) * (R // 2))
             nc.vector.tensor_copy(out=w3_grouped[:, half, :], in_=w3_raw[:, :, half].rearrange("p t r -> p r t"))
@@ -187,11 +187,11 @@ def tile_nonlocalmp_pb_kernel(tc, h2, feats, W3, b3, Wf, b_f, out):
             quantise_cols(*tiles[0], pair * PAIR_COLS, PAIR_COLS)
 
         feat_grouped = consts.tile([P, VIEWS * PACK], BF16, align_bytes=64, name="feat_grouped")
-        feat_codes = consts.tile([P, VIEWS], U32, align_bytes=64, name="feat_codes")
-        feat_scales = consts.tile([P, VIEWS], U8, align_bytes=64, name="feat_scales")
+        feat_codes = consts.tile([P, VIEWS], U32, align_bytes=256, name="feat_codes")
+        feat_scales = consts.tile([P, VIEWS], U8, align_bytes=256, name="feat_scales")
         wf_grouped = consts.tile([P, 2, O, PACK], BF16, align_bytes=64, name="wf_grouped")
-        wf_codes = consts.tile([P, 2, O], U32, align_bytes=64, name="wf_codes")
-        wf_scales = consts.tile([P, 2, O], U8, align_bytes=64, name="wf_scales")
+        wf_codes = consts.tile([P, 2, O], U32, align_bytes=256, name="wf_codes")
+        wf_scales = consts.tile([P, 2, O], U8, align_bytes=256, name="wf_scales")
 
         relu_sums = {}
         starts = {}
@@ -291,8 +291,8 @@ def tile_nonlocalmp_pb_kernel(tc, h2, feats, W3, b3, Wf, b_f, out):
             nc.scalar.mul(out=new_x(c, t)[:], in_=msum[:].rearrange("p m v -> p v m"), mul=RELU_WEIGHT)
 
         def quantise_msum(c, t):
-            x_codes = chunk_pool.tile([P, P], U32, align_bytes=64, name="x_codes")
-            x_scales = chunk_pool.tile([P, P], U8, align_bytes=64, name="x_scales")
+            x_codes = chunk_pool.tile([P, P], U32, align_bytes=256, name="x_codes")
+            x_scales = chunk_pool.tile([P, P], U8, align_bytes=256, name="x_scales")
             quantise(x_grouped[c, t][:].rearrange("p v m -> p (v m)"), x_codes[:], x_scales[:])
             x_quantised[c, t] = (x_codes, x_scales)
 
@@ -421,9 +421,10 @@ def tile_nonlocalmp_pb_kernel(tc, h2, feats, W3, b3, Wf, b_f, out):
         x_rows = new_x(c, 0)
         by_view = msum[:].rearrange("p m v -> p v m")
         nc.scalar.mul(out=x_rows[:, 0 : P // 2, :], in_=by_view[:, 0 : P // 2, :], mul=RELU_WEIGHT)
+        quantise_msum(c, 1)
+        fusion_msum(c, 1, out_banks[1])
         nc.vector.tensor_scalar_mul(out=x_rows[:, P // 2 : P, :], in0=by_view[:, P // 2 : P, :], scalar1=RELU_WEIGHT)
-        for t in reversed(range(VIEW_TILES)):
-            quantise_msum(c, t)
-            fusion_msum(c, t, out_banks[t])
+        quantise_msum(c, 0)
+        fusion_msum(c, 0, out_banks[0])
         for t in reversed(range(VIEW_TILES)):
             store_out(c, t, out_banks[t], 2 - t)

@@ -51,6 +51,10 @@ SCALAR_BLOCK = 1
 SCALAR_NEIGH = NEIGH // 2
 BANKS = [(0, m) for m in range(R_BLOCKS)] + [(1, m) for m in range(R_BLOCKS) if m != SCALAR_BLOCK] + [(1, SCALAR_BLOCK)]
 SCALAR_BANK = (0, SCALAR_BLOCK)
+EXTRA_BLOCK = 3
+EXTRA_UNITS = (LAST - 1, LAST)
+EXTRA_BANK = (0, EXTRA_BLOCK)
+EXTRA_BANKS = [(0, m) for m in range(R_BLOCKS)] + [(1, 0), (1, 2), (1, SCALAR_BLOCK), (1, EXTRA_BLOCK)]
 PAIRS = ROW_TILES // 2
 PAIR_COLS = 2 * P
 
@@ -114,8 +118,8 @@ def tile_nonlocalmp_pb_kernel(tc, h2, feats, W3, b3, Wf, b_f, out):
 
         def new_unit_tiles():
             grouped = grouped_pool.tile([P, UNIT_COLS * PACK], BF16, align_bytes=64, name="grouped")
-            codes = codes_pool.tile([P, UNIT_COLS], U32, align_bytes=256, name="codes")
-            scales = codes_pool.tile([P, UNIT_COLS], U8, align_bytes=256, name="scales")
+            codes = codes_pool.tile([P, UNIT_COLS], U32, align_bytes=64, name="codes")
+            scales = codes_pool.tile([P, UNIT_COLS], U8, align_bytes=64, name="scales")
             return grouped, codes, scales
 
         unit_offsets = [[(t * HALF_J + jj) * WORDS for t in range(VIEW_TILES)] for jj in range(HALF_J)]
@@ -157,13 +161,24 @@ def tile_nonlocalmp_pb_kernel(tc, h2, feats, W3, b3, Wf, b_f, out):
         bf_all = consts.tile([P, O], BF16, name="bf_all")
         nc.sync.dma_start(out=bf_all[:], in_=b_f.partition_broadcast(P))
 
+        zeros = consts.tile([P, BANK], BF16, name="zeros")
+        nc.vector.memset(zeros[:], 0.0)
+
+        def keep_busy(count):
+            idle_bank = psum_ring.tile([P, BANK], F32, tag="ring", name="idle_bank")
+            for k in range(count):
+                nc.tensor.matmul(out=idle_bank[:], lhsT=zeros[:, 0:P], rhs=zeros[:], start=True, stop=True)
+
+        keep_busy(5)
         tiles = {0: new_unit_tiles()}
         for pair in range(PAIRS):
             spread_pair(raws[0][pair // HALF_J], unit_offsets[pair % HALF_J], tiles[0][0], pair)
+            if pair == 1:
+                keep_busy(2)
 
         w3_grouped = consts.tile([P, R, PACK], BF16, align_bytes=64, name="w3_grouped")
-        w3_codes = consts.tile([P, R], U32, align_bytes=256, name="w3_codes")
-        w3_scales = consts.tile([P, R], U8, align_bytes=256, name="w3_scales")
+        w3_codes = consts.tile([P, R], U32, align_bytes=64, name="w3_codes")
+        w3_scales = consts.tile([P, R], U8, align_bytes=64, name="w3_scales")
         for h in range(2):
             half = slice(h * (R // 2), (h + 1) * (R // 2))
             nc.vector.tensor_copy(out=w3_grouped[:, half, :], in_=w3_raw[:, :, half].rearrange("p t r -> p r t"))
@@ -172,6 +187,7 @@ def tile_nonlocalmp_pb_kernel(tc, h2, feats, W3, b3, Wf, b_f, out):
         nc.vector.tensor_copy(out=b3_f32[:], in_=b3_rows[:])
         b3_bank = psum_ring.tile([P, P], F32, tag="ring", name="b3_bank")
         nc.tensor.transpose(b3_bank[:], b3_f32[:], ident[:])
+        keep_busy(2)
         quantise(w3_grouped[:].rearrange("p r t -> p (r t)"), w3_codes[:], w3_scales[:])
         quantise_cols(*tiles[0], PAIR_COLS, PAIR_COLS)
 
@@ -179,22 +195,25 @@ def tile_nonlocalmp_pb_kernel(tc, h2, feats, W3, b3, Wf, b_f, out):
         neg_b3 = consts.tile([P, R_BLOCKS], F32, name="neg_b3")
         seed_b3 = consts.tile([P, R_BLOCKS], F32, name="seed_b3")
         late_b3 = consts.tile([P, R_BLOCKS], F32, name="late_b3")
+        tail_b3 = consts.tile([P, R_BLOCKS], F32, name="tail_b3")
         nc.vector.tensor_copy(out=b3_cols[:], in_=b3_bank[:, 0:R_BLOCKS])
         nc.vector.tensor_scalar_mul(out=neg_b3[:], in0=b3_cols[:], scalar1=-1.0)
         nc.vector.tensor_scalar_mul(out=seed_b3[:], in0=b3_cols[:], scalar1=SEEDS - HALVES)
         nc.vector.tensor_scalar_mul(out=late_b3[:], in0=b3_cols[:], scalar1=SEEDS - SCALAR_NEIGH)
+        nc.vector.tensor_scalar_mul(out=tail_b3[:], in0=b3_cols[:], scalar1=SEEDS - HALVES - HALVES * len(EXTRA_UNITS))
         for pair in range(PAIRS // 2, PAIRS):
             quantise_cols(*tiles[0], pair * PAIR_COLS, PAIR_COLS)
 
         feat_grouped = consts.tile([P, VIEWS * PACK], BF16, align_bytes=64, name="feat_grouped")
-        feat_codes = consts.tile([P, VIEWS], U32, align_bytes=256, name="feat_codes")
-        feat_scales = consts.tile([P, VIEWS], U8, align_bytes=256, name="feat_scales")
+        feat_codes = consts.tile([P, VIEWS], U32, align_bytes=64, name="feat_codes")
+        feat_scales = consts.tile([P, VIEWS], U8, align_bytes=64, name="feat_scales")
         wf_grouped = consts.tile([P, 2, O, PACK], BF16, align_bytes=64, name="wf_grouped")
-        wf_codes = consts.tile([P, 2, O], U32, align_bytes=256, name="wf_codes")
-        wf_scales = consts.tile([P, 2, O], U8, align_bytes=256, name="wf_scales")
+        wf_codes = consts.tile([P, 2, O], U32, align_bytes=64, name="wf_codes")
+        wf_scales = consts.tile([P, 2, O], U8, align_bytes=64, name="wf_scales")
 
         relu_sums = {}
         starts = {}
+        tail_sums = {}
         waiting = []
         lin_banks = {}
         lin_rows = {}
@@ -220,7 +239,7 @@ def tile_nonlocalmp_pb_kernel(tc, h2, feats, W3, b3, Wf, b_f, out):
 
         def message_bank(u, i):
             c, g = divmod(u, UNITS_PER_CHUNK)
-            jp, m = BANKS[i]
+            jp, m = (EXTRA_BANKS if u in EXTRA_UNITS else BANKS)[i]
             codes_now, scales_now = tiles[u][1:]
             block = slice(m * P, (m + 1) * P)
             cols = slice(jp * BANK, (jp + 1) * BANK)
@@ -239,7 +258,7 @@ def tile_nonlocalmp_pb_kernel(tc, h2, feats, W3, b3, Wf, b_f, out):
             if starts_chunk:
                 starts[c, m] = relu_pool.tile([P, BANK], F32, tag="start", name="start")
                 nc.scalar.activation(out=starts[c, m][:], in_=main[:], func=ACT.Relu, bias=b3_cols[:, m : m + 1], scale=1.0)
-            elif (jp, m) == SCALAR_BANK:
+            elif (jp, m) == SCALAR_BANK or (u in EXTRA_UNITS and (jp, m) == EXTRA_BANK):
                 relu = relu_pool.tile([P, BANK], F32, name="relu")
                 nc.scalar.activation(out=relu[:], in_=main[:], func=ACT.Relu, bias=b3_cols[:, m : m + 1], scale=1.0)
                 nc.gpsimd.tensor_tensor(out=acc, in0=relu[:], in1=acc, op=ALU.add)
@@ -264,6 +283,15 @@ def tile_nonlocalmp_pb_kernel(tc, h2, feats, W3, b3, Wf, b_f, out):
                     op1=ALU.add,
                 )
 
+        def fold_tile(c, t, engine):
+            tail_sums[t] = chunk_pool.tile([P, R_BLOCKS, P], F32, tag="tail_sums%d" % t, name="tail_sums")
+            engine.tensor_tensor(
+                out=tail_sums[t][:],
+                in0=relu_sums[c][:, :, t * P : (t + 1) * P],
+                in1=relu_sums[c][:, :, CHUNK_VIEWS + t * P : CHUNK_VIEWS + (t + 1) * P],
+                op=ALU.add,
+            )
+
         def linear_transposes(c, t):
             lbank = psum_ring.tile([P, R_BLOCKS, P], F32, tag="ring", name="lbank")
             for m in range(R_BLOCKS):
@@ -274,25 +302,25 @@ def tile_nonlocalmp_pb_kernel(tc, h2, feats, W3, b3, Wf, b_f, out):
             x_grouped[c, t] = chunk_pool.tile([P, P, PACK], BF16, align_bytes=64, name="x_grouped")
             return x_grouped[c, t]
 
-        def add_linear(c, t):
+        def add_linear(c, t, sums):
             msum = chunk_pool.tile([P, R_BLOCKS, P], F32, name="msum")
             nc.vector.scalar_tensor_tensor(
                 out=msum[:],
                 in0=lin_cols[c, t][:],
                 scalar=LINEAR_OVER_RELU,
-                in1=folded[c][:, :, t * P : (t + 1) * P],
+                in1=sums,
                 op0=ALU.mult,
                 op1=ALU.add,
             )
             return msum
 
-        def combine(c, t):
-            msum = add_linear(c, t)
+        def combine(c, t, sums):
+            msum = add_linear(c, t, sums)
             nc.scalar.mul(out=new_x(c, t)[:], in_=msum[:].rearrange("p m v -> p v m"), mul=RELU_WEIGHT)
 
         def quantise_msum(c, t):
-            x_codes = chunk_pool.tile([P, P], U32, align_bytes=256, name="x_codes")
-            x_scales = chunk_pool.tile([P, P], U8, align_bytes=256, name="x_scales")
+            x_codes = chunk_pool.tile([P, P], U32, align_bytes=64, name="x_codes")
+            x_scales = chunk_pool.tile([P, P], U8, align_bytes=64, name="x_scales")
             quantise(x_grouped[c, t][:].rearrange("p v m -> p (v m)"), x_codes[:], x_scales[:])
             x_quantised[c, t] = (x_codes, x_scales)
 
@@ -355,6 +383,11 @@ def tile_nonlocalmp_pb_kernel(tc, h2, feats, W3, b3, Wf, b_f, out):
                             spread_pair(raws[w][pair // HALF_J], unit_offsets[pair % HALF_J], tiles[w][0], pair)
                 if i == 3 and finishing and g == 0:
                     fold(c - 1)
+                if u == LAST - 1 and i == 7:
+                    for m in range(R_BLOCKS):
+                        first = relu_sums[c][:, m, 0:CHUNK_VIEWS]
+                        seed = {SCALAR_BLOCK: late_b3, EXTRA_BLOCK: tail_b3}.get(m, seed_b3)[:, m : m + 1]
+                        nc.vector.tensor_scalar(out=first, in0=first, scalar1=seed, scalar2=None, op0=ALU.add)
                 if i == 5 and finishing and g == 1:
                     for t in range(VIEW_TILES):
                         quantise_msum(c - 1, t)
@@ -392,7 +425,7 @@ def tile_nonlocalmp_pb_kernel(tc, h2, feats, W3, b3, Wf, b_f, out):
             if finishing:
                 if g == 0:
                     for t in range(VIEW_TILES):
-                        combine(c - 1, t)
+                        combine(c - 1, t, folded[c - 1][:, :, t * P : (t + 1) * P])
                 if 0 < g <= VIEW_TILES:
                     out_bank = fusion_feats(c - 1, g - 1)
                     fusion_msum(c - 1, g - 1, out_bank)
@@ -406,18 +439,19 @@ def tile_nonlocalmp_pb_kernel(tc, h2, feats, W3, b3, Wf, b_f, out):
                 store_out(*waiting.pop(), 1)
         for i in range(ROW_TILES - 2, ROW_TILES):
             linear_pass(LAST, i)
-        for t in range(VIEW_TILES):
+        for t in reversed(range(VIEW_TILES)):
             linear_out_of_psum(c, t)
         for i in range(ROW_TILES - 2, ROW_TILES):
             message_bank(LAST, i)
+        for t in reversed(range(VIEW_TILES)):
+            linear_transposes(c, t)
         out_banks = []
         for t in range(VIEW_TILES):
             out_banks.append(fusion_feats(c, t))
-        for t in reversed(range(VIEW_TILES)):
-            linear_transposes(c, t)
-        fold(c)
-        combine(c, 1)
-        msum = add_linear(c, 0)
+        fold_tile(c, 0, nc.gpsimd)
+        fold_tile(c, 1, nc.vector)
+        combine(c, 1, tail_sums[1][:])
+        msum = add_linear(c, 0, tail_sums[0][:])
         x_rows = new_x(c, 0)
         by_view = msum[:].rearrange("p m v -> p v m")
         nc.scalar.mul(out=x_rows[:, 0 : P // 2, :], in_=by_view[:, 0 : P // 2, :], mul=RELU_WEIGHT)

from contextlib import ExitStack

import concourse.mybir as mybir
from concourse.masks import make_identity

F32 = mybir.dt.float32
BF16 = mybir.dt.bfloat16
U32 = mybir.dt.uint32
U8 = mybir.dt.uint8
FP8X4 = mybir.dt.float8_e4m3fn_x4
ALU = mybir.AluOpType
ACT = mybir.ActivationFunctionType

P = 128
PACK = 4
K_PASS = P * PACK
WORDS = K_PASS // 2

VIEWS = 1024
NEIGH = 16
Q = 512
R = 512
O = 512
NEG_SLOPE = 0.2

VIEW_TILES = 2
CHUNK_VIEWS = VIEW_TILES * P
N_CHUNKS = VIEWS // CHUNK_VIEWS
UNIT_J = 4
HALF_J = UNIT_J // 2
UNITS_PER_CHUNK = NEIGH // UNIT_J
N_UNITS = N_CHUNKS * UNITS_PER_CHUNK
ROW_TILES = VIEW_TILES * UNIT_J
UNIT_COLS = ROW_TILES * P
R_BLOCKS = R // P
BANK = 512
LOADS_AHEAD = 6
FT = {1:[0],2:[1],3:[2,3]}
WFQ = [(1, 6), (2, 3), (3, 3), (4, 3)]
TA = {0:[2],1:[4],2:[5],3:[6],4:[7],5:[8],6:[9],7:[10],8:[11],9:[12],10:[13],11:[14],12:[15]}
TM = {0:[1],1:[3]}
QA = {0:[1],1:[2],2:[3,4],3:[5],4:[6],5:[7],6:[8],7:[9],8:[10],9:[11],10:[12],11:[13],12:[14],13:[15]}
LAST = N_UNITS - 1
AHEAD = 2

RELU_WEIGHT = 1.0 - NEG_SLOPE
LINEAR_OVER_RELU = NEG_SLOPE / RELU_WEIGHT
SEEDS = NEIGH + NEIGH * LINEAR_OVER_RELU
HALVES = BANK // CHUNK_VIEWS
SCALAR_BLOCK = 1
SCALAR_NEIGH = NEIGH // 2
BANKS = [(0, m) for m in range(R_BLOCKS)] + [(1, m) for m in range(R_BLOCKS) if m != SCALAR_BLOCK] + [(1, SCALAR_BLOCK)]
SCALAR_BANK = (0, SCALAR_BLOCK)
EXTRA_BLOCK = 3
EXTRA_UNITS = (LAST - 1, LAST)
EXTRA_BANK = (0, EXTRA_BLOCK)
EXTRA_BANKS = [(0, m) for m in range(R_BLOCKS)] + [(1, 0), (1, 2), (1, SCALAR_BLOCK), (1, EXTRA_BLOCK)]
PAIRS = ROW_TILES // 2
PAIR_COLS = 2 * P

FLOPS = 2 * VIEWS * NEIGH * Q * R + 2 * VIEWS * (Q + R) * O


def tile_nonlocalmp_pb_kernel(tc, h2, feats, W3, b3, Wf, b_f, out):
    nc = tc.nc
    h2_rows = h2.rearrange("b i j k -> (b i) j k")
    feat_rows = feats.rearrange("b i k -> (b i) k")

    with ExitStack() as ctx:
        consts = ctx.enter_context(tc.tile_pool(name="consts", bufs=1))
        raw_pool = ctx.enter_context(tc.tile_pool(name="raw", bufs=LOADS_AHEAD + 1))
        grouped_pool = ctx.enter_context(tc.tile_pool(name="grouped", bufs=4))
        codes_pool = ctx.enter_context(tc.tile_pool(name="codes", bufs=4))
        chunk_pool = ctx.enter_context(tc.tile_pool(name="chunk", bufs=2))
        store_pool = ctx.enter_context(tc.tile_pool(name="store", bufs=3))
        relu_pool = ctx.enter_context(tc.tile_pool(name="relu", bufs=4))
        psum_ring = ctx.enter_context(tc.psum_pool(name="psum_ring", bufs=6))
        psum_lin = ctx.enter_context(tc.psum_pool(name="psum_lin", bufs=1))
        ctx.enter_context(tc.manual_schedule())

        def load_unit(u, between=None):
            c, g = divmod(u, UNITS_PER_CHUNK)
            views = slice(c * CHUNK_VIEWS, (c + 1) * CHUNK_VIEWS)
            halves = []
            for hf in range(2):
                raw = raw_pool.tile([P, VIEW_TILES, HALF_J * Q], BF16, tag="raw%d" % hf, name="raw")
                first_j = g * UNIT_J + hf * HALF_J
                nc.sync.dma_start(
                    out=raw[:],
                    in_=h2_rows[views, first_j : first_j + HALF_J, :].rearrange("(t p) j k -> p t (j k)", p=P),
                )
                halves.append(raw[:].rearrange("p t x -> p (t x)"))
                if between is not None and hf == 0:
                    between()
            return halves

        def spread_pair(raw, word_offsets, grouped, pair):
            raw_words = raw.bitcast(F32)
            grouped_words = grouped[:].bitcast(F32).rearrange("p (c u) -> p c u", u=2)
            bank = psum_ring.tile([P, 2, 2, P], F32, tag="ring", name="bank")
            for s in range(2):
                for u in range(2):
                    first = word_offsets[s] + u * P
                    nc.tensor.transpose(bank[:, s, u, :], raw_words[:, first : first + P], ident[:])
            nc.scalar.copy(
                out=grouped_words[:, pair * PAIR_COLS : (pair + 1) * PAIR_COLS, :].rearrange(
                    "p (s r) u -> p s r u", s=2
                ),
                in_=bank[:].rearrange("p s u r -> p s r u"),
            )

        def quantise(grouped_flat, codes_flat, scales_flat):
            nc.vector.quantize_mx(out=codes_flat.bitcast(FP8X4), scales=scales_flat, in_=grouped_flat)

        def quantise_cols(grouped, codes, scales, first, width):
            cols = slice(first, first + width)
            quantise(grouped[:, first * PACK : (first + width) * PACK], codes[:, cols], scales[:, cols])

        def new_unit_tiles():
            grouped = grouped_pool.tile([P, UNIT_COLS * PACK], BF16, align_bytes=64, name="grouped")
            codes = codes_pool.tile([P, UNIT_COLS], U32, align_bytes=64, name="codes")
            scales = codes_pool.tile([P, UNIT_COLS], U8, align_bytes=64, name="scales")
            return grouped, codes, scales

        unit_offsets = [[(t * HALF_J + jj) * WORDS for t in range(VIEW_TILES)] for jj in range(HALF_J)]
        feat_offsets = [[t * WORDS, (t + 1) * WORDS] for t in range(0, VIEWS // P, 2)]

        ident = consts.tile([P, P], F32, name="ident")
        make_identity(nc, ident[:])
        w3_raw = consts.tile([P, PACK, R], BF16, name="w3_raw")

        def load_w3():
            nc.sync.dma_start(
                out=w3_raw[:].rearrange("p (u e) r -> p u (e r)", e=2),
                in_=W3.rearrange("(u q e) r -> q u (e r)", u=2, e=2),
            )

        raws = {0: load_unit(0, load_w3)}
        b3_rows = consts.tile([P, P], BF16, name="b3_rows")
        nc.vector.memset(b3_rows[:], 0.0)
        nc.sync.dma_start(out=b3_rows[0:R_BLOCKS, :], in_=b3.rearrange("(m p) -> m p", p=P))
        raws[1] = load_unit(1)
        raws[2] = load_unit(2)
        raws[3] = load_unit(3)
        raws[4] = load_unit(4)
        feat_raw = consts.tile([P, VIEWS // P, Q], BF16, name="feat_raw")
        nc.sync.dma_start(
            out=feat_raw[:],
            in_=feat_rows.rearrange("(t p) k -> p t k", p=P),
        )
        wf_raw = consts.tile([P, 2, PACK, O], BF16, name="wf_raw")
        nc.sync.dma_start(
            out=wf_raw[:, 0, :, :].rearrange("p (u e) o -> p u (e o)", e=2),
            in_=Wf[0:K_PASS, :].rearrange("(u q e) o -> q u (e o)", u=2, e=2),
        )
        nc.sync.dma_start(
            out=wf_raw[:, 1, :, :],
            in_=Wf[K_PASS : 2 * K_PASS, :].rearrange("(t p) o -> p t o", p=P),
        )
        raws[5] = load_unit(5)
        bf_all = consts.tile([P, O], BF16, name="bf_all")
        nc.sync.dma_start(out=bf_all[:], in_=b_f.partition_broadcast(P))

        zeros = consts.tile([P, BANK], BF16, name="zeros")
        nc.vector.memset(zeros[:], 0.0)

        def keep_busy(count):
            idle_bank = psum_ring.tile([P, BANK], F32, tag="ring", name="idle_bank")
            for k in range(count):
                nc.tensor.matmul(out=idle_bank[:], lhsT=zeros[:, 0:P], rhs=zeros[:], start=True, stop=True)

        keep_busy(5)
        tiles = {0: new_unit_tiles()}
        for pair in range(PAIRS):
            spread_pair(raws[0][pair // HALF_J], unit_offsets[pair % HALF_J], tiles[0][0], pair)
            if pair == 1:
                keep_busy(2)

        w3_grouped = consts.tile([P, R, PACK], BF16, align_bytes=64, name="w3_grouped")
        w3_codes = consts.tile([P, R], U32, align_bytes=64, name="w3_codes")
        w3_scales = consts.tile([P, R], U8, align_bytes=64, name="w3_scales")
        for h in range(2):
            half = slice(h * (R // 2), (h + 1) * (R // 2))
            nc.vector.tensor_copy(out=w3_grouped[:, half, :], in_=w3_raw[:, :, half].rearrange("p t r -> p r t"))
        quantise_cols(*tiles[0], 0, PAIR_COLS)
        b3_f32 = consts.tile([P, P], F32, name="b3_f32")
        nc.vector.tensor_copy(out=b3_f32[:], in_=b3_rows[:])
        b3_bank = psum_ring.tile([P, P], F32, tag="ring", name="b3_bank")
        nc.tensor.transpose(b3_bank[:], b3_f32[:], ident[:])
        keep_busy(2)
        quantise(w3_grouped[:].rearrange("p r t -> p (r t)"), w3_codes[:], w3_scales[:])
        quantise_cols(*tiles[0], PAIR_COLS, PAIR_COLS)

        b3_cols = consts.tile([P, R_BLOCKS], F32, name="b3_cols")
        neg_b3 = consts.tile([P, R_BLOCKS], F32, name="neg_b3")
        seed_b3 = consts.tile([P, R_BLOCKS], F32, name="seed_b3")
        late_b3 = consts.tile([P, R_BLOCKS], F32, name="late_b3")
        tail_b3 = consts.tile([P, R_BLOCKS], F32, name="tail_b3")
        nc.vector.tensor_copy(out=b3_cols[:], in_=b3_bank[:, 0:R_BLOCKS])
        nc.vector.tensor_scalar_mul(out=neg_b3[:], in0=b3_cols[:], scalar1=-1.0)
        nc.vector.tensor_scalar_mul(out=seed_b3[:], in0=b3_cols[:], scalar1=SEEDS - HALVES)
        nc.vector.tensor_scalar_mul(out=late_b3[:], in0=b3_cols[:], scalar1=SEEDS - SCALAR_NEIGH)
        nc.vector.tensor_scalar_mul(out=tail_b3[:], in0=b3_cols[:], scalar1=SEEDS - HALVES - HALVES * len(EXTRA_UNITS))
        for pair in range(PAIRS // 2, PAIRS):
            quantise_cols(*tiles[0], pair * PAIR_COLS, PAIR_COLS)

        feat_grouped = consts.tile([P, VIEWS * PACK], BF16, align_bytes=64, name="feat_grouped")
        feat_codes = consts.tile([P, VIEWS], U32, align_bytes=64, name="feat_codes")
        feat_scales = consts.tile([P, VIEWS], U8, align_bytes=64, name="feat_scales")
        wf_grouped = consts.tile([P, 2, O, PACK], BF16, align_bytes=64, name="wf_grouped")
        wf_codes = consts.tile([P, 2, O], U32, align_bytes=64, name="wf_codes")
        wf_scales = consts.tile([P, 2, O], U8, align_bytes=64, name="wf_scales")

        relu_sums = {}
        starts = {}
        tail_sums = {}
        waiting = []
        lin_banks = {}
        lin_rows = {}
        folded = {}
        lin_cols = {}
        x_grouped = {}
        x_quantised = {}

        def linear_pass(u, i):
            c, g = divmod(u, UNITS_PER_CHUNK)
            codes, scales = tiles[u][1:]
            jj, t = divmod(i, VIEW_TILES)
            piece = slice(i * P, (i + 1) * P)
            nc.tensor.matmul_mx(
                out=lin_banks[c][t][:],
                lhsT=codes[:, piece].bitcast(FP8X4),
                lhsT_scale=scales[:, piece],
                rhs=w3_codes[:].bitcast(FP8X4),
                rhs_scale=w3_scales[:],
                start=(g == 0 and jj == 0),
                stop=(g == UNITS_PER_CHUNK - 1 and jj == UNIT_J - 1),
            )

        def message_bank(u, i):
            c, g = divmod(u, UNITS_PER_CHUNK)
            jp, m = (EXTRA_BANKS if u in EXTRA_UNITS else BANKS)[i]
            codes_now, scales_now = tiles[u][1:]
            block = slice(m * P, (m + 1) * P)
            cols = slice(jp * BANK, (jp + 1) * BANK)
            starts_chunk = g == 0 and jp == 0
            main = psum_ring.tile([P, BANK], F32, tag="ring", name="main")
            nc.tensor.matmul_mx(
                out=main[:],
                lhsT=w3_codes[:, block].bitcast(FP8X4),
                lhsT_scale=w3_scales[:, block],
                rhs=codes_now[:, cols].bitcast(FP8X4),
                rhs_scale=scales_now[:, cols],
                start=True,
                stop=True,
            )
            acc = relu_sums[c][:, m, :]
            if starts_chunk:
                starts[c, m] = relu_pool.tile([P, BANK], F32, tag="start", name="start")
                nc.scalar.activation(out=starts[c, m][:], in_=main[:], func=ACT.Relu, bias=b3_cols[:, m : m + 1], scale=1.0)
            elif (jp, m) == SCALAR_BANK or (u in EXTRA_UNITS and (jp, m) == EXTRA_BANK):
                relu = relu_pool.tile([P, BANK], F32, name="relu")
                nc.scalar.activation(out=relu[:], in_=main[:], func=ACT.Relu, bias=b3_cols[:, m : m + 1], scale=1.0)
                nc.gpsimd.tensor_tensor(out=acc, in0=relu[:], in1=acc, op=ALU.add)
            else:
                before = starts[c, m][:] if g == 0 and jp == 1 else acc
                nc.vector.scalar_tensor_tensor(
                    out=acc, in0=main[:], scalar=neg_b3[:, m : m + 1], in1=before, op0=ALU.max, op1=ALU.add
                )
        def linear_out_of_psum(c, t):
            nc.scalar.copy(out=lin_rows[c][:, t, :], in_=lin_banks[c][t][:])

        def fold(c):
            folded[c] = chunk_pool.tile([P, R_BLOCKS, CHUNK_VIEWS], F32, name="folded")
            for m in range(R_BLOCKS):
                sums = relu_sums[c][:, m, :]
                nc.vector.scalar_tensor_tensor(
                    out=folded[c][:, m, :],
                    in0=sums[:, 0:CHUNK_VIEWS],
                    scalar=(late_b3 if m == SCALAR_BLOCK else seed_b3)[:, m : m + 1],
                    in1=sums[:, CHUNK_VIEWS : 2 * CHUNK_VIEWS],
                    op0=ALU.add,
                    op1=ALU.add,
                )

        def fold_tile(c, t, engine):
            tail_sums[t] = chunk_pool.tile([P, R_BLOCKS, P], F32, tag="tail_sums%d" % t, name="tail_sums")
            engine.tensor_tensor(
                out=tail_sums[t][:],
                in0=relu_sums[c][:, :, t * P : (t + 1) * P],
                in1=relu_sums[c][:, :, CHUNK_VIEWS + t * P : CHUNK_VIEWS + (t + 1) * P],
                op=ALU.add,
            )

        def linear_transposes(c, t):
            lbank = psum_ring.tile([P, R_BLOCKS, P], F32, tag="ring", name="lbank")
            for m in range(R_BLOCKS):
                nc.tensor.transpose(lbank[:, m, :], lin_rows[c][:, t, m * P : (m + 1) * P], ident[:])
            lin_cols[c, t] = lbank

        def new_x(c, t):
            x_grouped[c, t] = chunk_pool.tile([P, P, PACK], BF16, align_bytes=64, name="x_grouped")
            return x_grouped[c, t]

        def add_linear(c, t, sums):
            msum = chunk_pool.tile([P, R_BLOCKS, P], F32, name="msum")
            nc.vector.scalar_tensor_tensor(
                out=msum[:],
                in0=lin_cols[c, t][:],
                scalar=LINEAR_OVER_RELU,
                in1=sums,
                op0=ALU.mult,
                op1=ALU.add,
            )
            return msum

        def combine(c, t, sums):
            msum = add_linear(c, t, sums)
            nc.scalar.mul(out=new_x(c, t)[:], in_=msum[:].rearrange("p m v -> p v m"), mul=RELU_WEIGHT)

        def quantise_msum(c, t):
            x_codes = chunk_pool.tile([P, P], U32, align_bytes=64, name="x_codes")
            x_scales = chunk_pool.tile([P, P], U8, align_bytes=64, name="x_scales")
            quantise(x_grouped[c, t][:].rearrange("p v m -> p (v m)"), x_codes[:], x_scales[:])
            x_quantised[c, t] = (x_codes, x_scales)

        def fusion_feats(c, t):
            first = c * CHUNK_VIEWS + t * P
            out_bank = psum_ring.tile([P, O], F32, tag="ring", name="out_bank")
            nc.tensor.matmul_mx(
                out=out_bank[:],
                lhsT=feat_codes[:, first : first + P].bitcast(FP8X4),
                lhsT_scale=feat_scales[:, first : first + P],
                rhs=wf_codes[:, 0, :].bitcast(FP8X4),
                rhs_scale=wf_scales[:, 0, :],
                start=True,
                stop=False,
            )
            return out_bank

        def fusion_msum(c, t, out_bank):
            x_codes, x_scales = x_quantised[c, t]
            nc.tensor.matmul_mx(
                out=out_bank[:],
                lhsT=x_codes[:].bitcast(FP8X4),
                lhsT_scale=x_scales[:],
                rhs=wf_codes[:, 1, :].bitcast(FP8X4),
                rhs_scale=wf_scales[:, 1, :],
                start=False,
                stop=True,
            )

        def store_out(c, t, out_bank, pieces):
            first = c * CHUNK_VIEWS + t * P
            for k in range(pieces):
                cols = slice(k * O // pieces, (k + 1) * O // pieces)
                result = store_pool.tile([P, O // pieces], F32, tag="result%d" % pieces, name="result")
                nc.vector.tensor_tensor(out=result[:], in0=out_bank[:, cols], in1=bf_all[:, cols], op=ALU.add)
                nc.sync.dma_start(out=out[first : first + P, cols], in_=result[:])

        for u in range(LAST):
            c, g = divmod(u, UNITS_PER_CHUNK)
            if u + LOADS_AHEAD < N_UNITS:
                raws[u + LOADS_AHEAD] = load_unit(u + LOADS_AHEAD)
            if g == 0:
                relu_sums[c] = chunk_pool.tile([P, R_BLOCKS, BANK], F32, name="relu_sums")
                lin_rows[c] = chunk_pool.tile([P, VIEW_TILES, R], F32, name="lin_rows")
                lin_banks[c] = []
                for t in range(VIEW_TILES):
                    lin_bank = psum_lin.tile([P, R], F32, tag="lin%d" % t, name="lin%d" % t)
                    lin_banks[c].append(lin_bank)
            finishing = c > 0

            for i in range(ROW_TILES):
                message_bank(u, i)
                linear_pass(u, i)
                if i == 1 and waiting:
                    store_out(*waiting.pop(), 1)
                if i == R_BLOCKS - 1:
                    for w in TM.get(u, ()):
                        tiles[w] = new_unit_tiles()
                        for pair in range(PAIRS):
                            spread_pair(raws[w][pair // HALF_J], unit_offsets[pair % HALF_J], tiles[w][0], pair)
                if i == 3 and finishing and g == 0:
                    fold(c - 1)
                if u == LAST - 1 and i == 7:
                    for m in range(R_BLOCKS):
                        first = relu_sums[c][:, m, 0:CHUNK_VIEWS]
                        seed = {SCALAR_BLOCK: late_b3, EXTRA_BLOCK: tail_b3}.get(m, seed_b3)[:, m : m + 1]
                        nc.vector.tensor_scalar(out=first, in0=first, scalar1=seed, scalar2=None, op0=ALU.add)
                if i == 5 and finishing and g == 1:
                    for t in range(VIEW_TILES):
                        quantise_msum(c - 1, t)
                if (u, i) in WFQ:
                    s, h = divmod(WFQ.index((u, i)), 2)
                    half = slice(h * (O // 2), (h + 1) * (O // 2))
                    nc.scalar.copy(
                        out=wf_grouped[:, s, half, :], in_=wf_raw[:, s, :, half].rearrange("p t o -> p o t")
                    )

            ends_chunk = g == UNITS_PER_CHUNK - 1
            if ends_chunk:
                linear_out_of_psum(c, 0)
            for w in TA.get(u, ()):
                tiles[w] = new_unit_tiles()
                for pair in range(PAIRS):
                    spread_pair(raws[w][pair // HALF_J], unit_offsets[pair % HALF_J], tiles[w][0], pair)
                    if ends_chunk and pair == 1:
                        linear_out_of_psum(c, 1)
            for k in FT.get(u, ()):
                spread_pair(feat_raw[:].rearrange("p t k -> p (t k)"), feat_offsets[k], feat_grouped, k)
            if finishing and g == 0:
                for t in range(VIEW_TILES):
                    linear_transposes(c - 1, t)

            for w in QA.get(u, ()):
                for h in range(HALVES):
                    quantise_cols(*tiles[w], h * BANK, BANK)

            for k in FT.get(u - 1, ()):
                quantise_cols(feat_grouped, feat_codes, feat_scales, k * PAIR_COLS, PAIR_COLS)
            if u == 3 or u == 4:
                s = u - 3
                quantise(wf_grouped[:, s, :, :].rearrange("p o t -> p (o t)"), wf_codes[:, s, :], wf_scales[:, s, :])
            if finishing:
                if g == 0:
                    for t in range(VIEW_TILES):
                        combine(c - 1, t, folded[c - 1][:, :, t * P : (t + 1) * P])
                if 0 < g <= VIEW_TILES:
                    out_bank = fusion_feats(c - 1, g - 1)
                    fusion_msum(c - 1, g - 1, out_bank)
                    waiting.append((c - 1, g - 1, out_bank))

        c = N_CHUNKS - 1
        for i in range(ROW_TILES - 2):
            message_bank(LAST, i)
            linear_pass(LAST, i)
            if i == 1:
                store_out(*waiting.pop(), 1)
        for i in range(ROW_TILES - 2, ROW_TILES):
            linear_pass(LAST, i)
        for t in reversed(range(VIEW_TILES)):
            linear_out_of_psum(c, t)
        for i in range(ROW_TILES - 2, ROW_TILES):
            message_bank(LAST, i)
        for t in reversed(range(VIEW_TILES)):
            linear_transposes(c, t)
        out_banks = []
        for t in range(VIEW_TILES):
            out_banks.append(fusion_feats(c, t))
        fold_tile(c, 0, nc.gpsimd)
        fold_tile(c, 1, nc.vector)
        combine(c, 1, tail_sums[1][:])
        msum = add_linear(c, 0, tail_sums[0][:])
        x_rows = new_x(c, 0)
        by_view = msum[:].rearrange("p m v -> p v m")
        nc.scalar.mul(out=x_rows[:, 0 : P // 2, :], in_=by_view[:, 0 : P // 2, :], mul=RELU_WEIGHT)
        quantise_msum(c, 1)
        fusion_msum(c, 1, out_banks[1])
        nc.vector.tensor_scalar_mul(out=x_rows[:, P // 2 : P, :], in0=by_view[:, P // 2 : P, :], scalar1=RELU_WEIGHT)
        quantise_msum(c, 0)
        fusion_msum(c, 0, out_banks[0])
        for t in reversed(range(VIEW_TILES)):
            store_out(c, t, out_banks[t], 2 - t)
